import numpy as np
import ml_dtypes


def mxq(x, axis, fmt="e4m3"):
    dtype, down = {"e4m3": (ml_dtypes.float8_e4m3fn, 7), "e5m2": (ml_dtypes.float8_e5m2, 14)}[fmt]
    v = np.moveaxis(np.asarray(x, np.float32).astype(ml_dtypes.bfloat16).astype(np.float64), axis, -1)
    blocks = v.reshape(v.shape[:-1] + (-1, 32))
    amax = np.abs(blocks).max(-1, keepdims=True)
    byte = np.maximum(np.where(amax > 0, np.frexp(amax)[1] - 1 + 127, 0) - down, 1)
    scale = np.exp2(byte - 127.0)
    codes = (blocks / scale).astype(np.float32).astype(dtype).astype(np.float64)
    return np.moveaxis((codes * scale).reshape(v.shape), -1, axis)


WIDE = False


def mx_kscale(k):
    if not WIDE:
        return np.ones(k)
    levels = np.array([10, -10, 5, -5, 0])
    if k % 512:
        return np.exp2(np.random.permutation(np.resize(levels, k // 32))).repeat(32)
    a = np.empty((k // 512, 16))
    for p in range(k // 512):
        a[p, :8] = np.random.permutation(np.resize(levels, 8))
        for g in range(8):
            far = levels[np.abs(levels - a[p, g]) >= 10]
            a[p, g + 8] = far[np.random.randint(len(far))]
    return np.exp2(a.ravel()).repeat(32)


BF16 = ml_dtypes.bfloat16


def bf(x):
    return np.asarray(x, np.float32).astype(BF16)


def f64(x):
    return np.asarray(x).astype(np.float64)


B, T, E, H, FF = 4, 1024, 1024, 8, 512
EPS = 1e-5


def layernorm(r, g):
    mu = r.mean(-1, keepdims=True)
    var = ((r - mu) ** 2).mean(-1, keepdims=True)
    return (r - mu) / np.sqrt(var + EPS) * g


def setup_inputs():
    t = mx_kscale(FF)
    z = np.random.standard_normal((B, T, FF))
    return {
        "y_act": bf(z * z / (1.0 + np.exp(-z)) * t),
        "h": bf(np.random.standard_normal((B, T, E))),
        "W2": bf(np.random.standard_normal((FF, E)) / np.sqrt(FF) / t[:, None]),
        "b2": bf(np.random.standard_normal(E) * 0.1),
        "g2": bf(1.0 + np.random.standard_normal(E) * 0.1),
    }


def core(y_act, h, W2, b2, g2):
    ff = (mxq(f64(y_act), 2, "e4m3") @ mxq(f64(W2), 0, "e4m3")) + f64(b2)
    return layernorm(ff + f64(h), f64(g2))


def e4m3fn_bytes(y):
    return np.clip(np.asarray(y, np.float64), -448.0, 448.0).astype(np.float32).astype(ml_dtypes.float8_e4m3fn).view(np.uint8)


def reference(y_act, h, W2, b2, g2):
    out = core(y_act, h, W2, b2, g2)
    s = np.max(np.abs(out), axis=-1, keepdims=True) / 448.0
    return out, e4m3fn_bytes(out / s)

@@ -1,0 +1,395 @@
+from contextlib import ExitStack
+
+import concourse.mybir as mybir
+from concourse.masks import make_identity
+
+FLOPS = 2 * 4096 * 512 * 1024
+
+F32 = mybir.dt.float32
+BF16 = mybir.dt.bfloat16
+U32 = mybir.dt.uint32
+U8 = mybir.dt.uint8
+FP8X4 = mybir.dt.float8_e4m3fn_x4
+FP8 = mybir.dt.float8_e4m3fn
+ALU = mybir.AluOpType
+ACT = mybir.ActivationFunctionType
+AX = mybir.AxisListType
+
+P = 128
+K = 512
+PACK = 4
+N = 1024
+BANK = 512
+EPS = 1e-5
+TILES = 32
+QUAD = 4
+QUADS = TILES // QUAD
+
+W_VECTOR_COLS = 320
+POOL_SCALES_FROM = 20
+VECTOR_COLS = {10: 256, 11: 704}
+QUANTIZE_SLOT = 3
+ADDS_BEFORE_PARK = 1
+
+
+def tile_transformerblock_pb_t_kernel(tc, y_act, h, W2, b2, g2, out_0, out_1):
+    nc = tc.nc
+    y_quads = y_act.flatten_outer_dims().rearrange("(q p j) k -> q p j k", p=P, j=QUAD)
+    h_quads = h.flatten_outer_dims().rearrange("(q p j) n -> q p j n", p=P, j=QUAD)
+    out_0_quads = out_0.flatten_outer_dims().rearrange("(q p j) n -> q p j n", p=P, j=QUAD)
+    out_1_quads = out_1.flatten_outer_dims().rearrange("(q p j) n -> q p j n", p=P, j=QUAD)
+
+    groups = [[0], [1], [2, 3]] + [list(range(QUAD * q, QUAD * q + QUAD)) for q in range(1, 7)] + [[28, 29], [30], [31]]
+    units = [(0, 1), (1, 2), (2, 4)] + [(QUAD * q, QUAD * q + QUAD) for q in range(1, QUADS)]
+    unit_of = {}
+    for u in range(len(units)):
+        for i in range(units[u][0], units[u][1]):
+            unit_of[i] = u
+
+    with ExitStack() as ctx:
+        const = ctx.enter_context(tc.tile_pool(name="const", bufs=1))
+        y_pool = ctx.enter_context(tc.tile_pool(name="y_pool", bufs=4))
+        grouped_pool = ctx.enter_context(tc.tile_pool(name="grouped_pool", bufs=4))
+        codes_pool = ctx.enter_context(tc.tile_pool(name="codes_pool", bufs=4))
+        h_pool = ctx.enter_context(tc.tile_pool(name="h_pool", bufs=3))
+        r_pool = ctx.enter_context(tc.tile_pool(name="r_pool", bufs=12))
+        t_pool = ctx.enter_context(tc.tile_pool(name="t_pool", bufs=12))
+        bytes_pool = ctx.enter_context(tc.tile_pool(name="bytes_pool", bufs=3))
+        squares_pool = ctx.enter_context(tc.tile_pool(name="squares_pool", bufs=2))
+        g2_psum = ctx.enter_context(tc.psum_pool(name="g2_psum", bufs=1))
+        mm_psum = ctx.enter_context(tc.psum_pool(name="mm_psum", bufs=5))
+        turn_psum = ctx.enter_context(tc.psum_pool(name="turn_psum", bufs=2))
+        ctx.enter_context(tc.manual_schedule())
+
+        y_rows = {}
+        y_grouped = {}
+        y_codes = {}
+        y_scales = {}
+        h_rows = {}
+        r_tiles = {}
+        t_tiles = {}
+        byte_tiles = {}
+
+        half_sums = const.tile([P, 2 * TILES], F32, name="half_sums", tag="half_sums")
+        row_sums = const.tile([P, TILES], F32, name="row_sums", tag="row_sums")
+        neg_mean = const.tile([P, TILES], F32, name="neg_mean", tag="neg_mean")
+        sq_sums = const.tile([P, TILES], F32, name="sq_sums", tag="sq_sums")
+        std = const.tile([P, TILES], F32, name="std", tag="std")
+        trio = const.tile([P, TILES, 3], F32, name="trio", tag="trio")
+        q_scale = const.tile([P, TILES], F32, name="q_scale", tag="q_scale")
+        factor = const.tile([P, TILES], F32, name="factor", tag="factor")
+        unused_sum = const.tile([P, 1], F32, name="unused_sum", tag="unused_sum")
+        unused_pair = const.tile([P, 2], F32, name="unused_pair", tag="unused_pair")
+
+        def span(g):
+            return groups[g][0], groups[g][-1] + 1
+
+        def load_y(u):
+            a, z = units[u]
+            y_rows[u] = y_pool.tile([P, z - a, K], BF16, name="y_rows", tag="y_rows")
+            nc.sync.dma_start(out=y_rows[u][:], in_=y_quads[a // QUAD][:, a % QUAD : a % QUAD + z - a, :])
+
+        def load_h(q, j0, j1):
+            if j0 == 0:
+                h_rows[q] = h_pool.tile([P, QUAD, N], BF16, name="h_rows", tag="h_rows")
+            nc.sync.dma_start(out=h_rows[q][:, j0:j1, :], in_=h_quads[q][:, j0:j1, :])
+
+        def turn_y(u):
+            a, z = units[u]
+            y_grouped[u] = grouped_pool.tile([P, QUAD * K], BF16, name="y_grouped", tag="y_grouped", align_bytes=64)
+            for j0 in range(0, z - a, 2):
+                nj = min(2, z - a - j0)
+                turned = turn_psum.tile([P, 2, 2, P], F32, name="turned", tag="turned")
+                for j in range(nj):
+                    words = y_rows[u][:, j0 + j, :].bitcast(F32)
+                    for e in range(2):
+                        nc.tensor.transpose(turned[:, j, e, :], words[:, e : K // 2 : 2], identity[:])
+                nc.scalar.copy(
+                    out=y_grouped[u][:, j0 * K : (j0 + nj) * K].bitcast(F32).rearrange("p (j r e) -> p j r e", j=nj, e=2),
+                    in_=turned[:, 0:nj, :, :].rearrange("p j e r -> p j r e"),
+                )
+
+        def quantize_y(u):
+            a, z = units[u]
+            y_codes[u] = codes_pool.tile([P, QUAD * P], U32, name="y_codes", tag="y_codes", align_bytes=64)
+            y_scales[u] = codes_pool.tile([P, QUAD * P], U8, name="y_scales", tag="y_scales", align_bytes=64)
+            nc.vector.quantize_mx(
+                out=y_codes[u][:, 0 : (z - a) * P].bitcast(FP8X4),
+                scales=y_scales[u][:, 0 : (z - a) * P],
+                in_=y_grouped[u][:, 0 : (z - a) * K],
+            )
+
+        def park_pool(u):
+            nc.gpsimd.tensor_copy(out=parked[:, 0:1], in_=y_codes[u][:, 0:1])
+
+        def add_bias(i):
+            r_tiles[i] = r_pool.tile([P, N], F32, name="r_tile", tag="r_tile")
+            nc.gpsimd.tensor_tensor(out=r_tiles[i][:], in0=h_rows[i // QUAD][:, i % QUAD, :], in1=b2_rows[:], op=ALU.add)
+
+        def matmul_residual(i, b):
+            u = unit_of[i]
+            rows = slice((i - units[u][0]) * P, (i - units[u][0] + 1) * P)
+            cols = slice(b * BANK, (b + 1) * BANK)
+            product = mm_psum.tile([P, BANK], F32, name="product", tag="product")
+            nc.tensor.matmul_mx(
+                out=product[:],
+                lhsT=y_codes[u][:, rows].bitcast(FP8X4),
+                lhsT_scale=y_scales[u][:, rows],
+                rhs=w_codes[:, cols].bitcast(FP8X4),
+                rhs_scale=w_scales[:, cols],
+                start=True,
+                stop=True,
+            )
+            nc.vector.scalar_tensor_tensor(
+                out=r_tiles[i][:, cols],
+                in0=product[:],
+                scalar=1.0,
+                in1=r_tiles[i][:, cols],
+                op0=ALU.mult,
+                op1=ALU.add,
+                accum_out=half_sums[:, 2 * i + b : 2 * i + b + 1],
+            )
+
+        def add_half_sums(g):
+            a, z = span(g)
+            if z - a > 1:
+                nc.vector.tensor_reduce(
+                    out=row_sums[:, a:z],
+                    in_=half_sums[:, 2 * a : 2 * z].rearrange("p (i b) -> p i b", b=2),
+                    axis=AX.X,
+                    op=ALU.add,
+                )
+
+        def negate_mean(g):
+            a, z = span(g)
+            if z - a > 1:
+                nc.vector.tensor_scalar(
+                    out=neg_mean[:, a:z], in0=row_sums[:, a:z], scalar1=-1.0 / N, scalar2=None, op0=ALU.mult, op1=ALU.add,
+                    accum_out=unused_sum[:, 0:1],
+                )
+            else:
+                nc.vector.tensor_scalar(
+                    out=unused_pair[:], in0=half_sums[:, 2 * a : 2 * a + 2], scalar1=-1.0 / N, scalar2=None, op0=ALU.mult,
+                    op1=ALU.add, accum_out=neg_mean[:, a : a + 1],
+                )
+
+        def square_deviation(i):
+            squares = squares_pool.tile([P, N], BF16, name="squares", tag="squares")
+            nc.scalar.activation(
+                out=squares[:], in_=r_tiles[i][:], func=ACT.Square, bias=neg_mean[:, i : i + 1], scale=1.0,
+                accum_out=sq_sums[:, i : i + 1],
+            )
+
+        def root(g):
+            a, z = span(g)
+            nc.scalar.activation(out=std[:, a:z], in_=sq_sums[:, a:z], func=ACT.Sqrt, bias=EPS, scale=1.0 / N)
+
+        def invert_std(g):
+            a, z = span(g)
+            nc.vector.reciprocal(out=trio[:, a:z, 1], in_=std[:, a:z])
+
+        def gain(i):
+            t_tiles[i] = t_pool.tile([P, N], F32, name="t_tile", tag="t_tile")
+            nc.vector.scalar_tensor_tensor(
+                out=t_tiles[i][:], in0=r_tiles[i][:], scalar=neg_mean[:, i : i + 1], in1=g2_rows[:], op0=ALU.add, op1=ALU.mult,
+            )
+
+        def row_amax(i):
+            nc.vector.tensor_reduce(out=trio[:, i, 0:1], in_=t_tiles[i][:], axis=AX.X, op=ALU.max, apply_absolute_value=True)
+
+        def scale_of_rows(g):
+            a, z = span(g)
+            nc.vector.tensor_reduce(out=q_scale[:, a:z], in_=trio[:, a:z, :], axis=AX.X, op=ALU.mult)
+
+        def invert_scale(g):
+            a, z = span(g)
+            nc.vector.reciprocal(out=factor[:, a:z], in_=q_scale[:, a:z])
+
+        def scale_on_pool(i):
+            nc.gpsimd.tensor_scalar(
+                out=t_tiles[i][:], in0=t_tiles[i][:], scalar1=trio[:, i, 1:2], scalar2=1.0, op0=ALU.mult, op1=ALU.mult,
+            )
+
+        def pool_scales(i):
+            return POOL_SCALES_FROM <= i < TILES - 1
+
+        def finish(g, i):
+            a, z = span(g)
+            t = t_tiles[i]
+            c = VECTOR_COLS.get(g, 0)
+            if i == a:
+                byte_tiles[g] = bytes_pool.tile([P, z - a, N], FP8, name="byte_tile", tag="byte_tile")
+            if not pool_scales(i):
+                if c:
+                    nc.vector.tensor_scalar(out=t[:, 0:c], in0=t[:, 0:c], scalar1=trio[:, i, 1:2], scalar2=None, op0=ALU.mult)
+                nc.scalar.activation(out=t[:, c:N], in_=t[:, c:N], func=ACT.Copy, scale=trio[:, i, 1:2])
+            nc.sync.dma_start(out=out_0_quads[i // QUAD][:, i % QUAD, :], in_=t[:])
+            if c:
+                nc.vector.tensor_scalar(
+                    out=byte_tiles[g][:, i - a, 0:c], in0=t[:, 0:c], scalar1=factor[:, i : i + 1], scalar2=None, op0=ALU.mult,
+                    saturate=False,
+                )
+            nc.scalar.activation(
+                out=byte_tiles[g][:, i - a, c:N], in_=t[:, c:N], func=ACT.Identity, scale=factor[:, i : i + 1],
+                bias=zeros[:, 0:1], saturate=False,
+            )
+            if i == z - 1:
+                nc.sync.dma_start(
+                    out=out_1_quads[i // QUAD][:, a % QUAD : a % QUAD + z - a, :], in_=byte_tiles[g][:].bitcast(U8),
+                )
+
+        vectors = const.tile([P, 2 * N], BF16, name="vectors", tag="vectors")
+        nc.vector.memset(vectors[:].bitcast(F32), 0.0)
+        ones = const.tile([P, P], BF16, name="ones", tag="ones")
+        nc.vector.memset(ones[:], 1.0)
+        zeros = const.tile([P, TILES], F32, name="zeros", tag="zeros")
+        nc.vector.memset(zeros[:], 0.0)
+        one = const.tile([P, 1], F32, name="one", tag="one")
+        nc.vector.memset(one[:], 1.0)
+        warmed = const.tile([P, 1], F32, name="warmed", tag="warmed")
+        nc.scalar.activation(out=warmed[:], in_=one[:], func=ACT.Sqrt)
+        nc.vector.tensor_scalar(out=trio[:, :, 2], in0=zeros[:], scalar1=1.0, scalar2=1.0 / 448.0, op0=ALU.mult, op1=ALU.add)
+        identity = const.tile([P, P], F32, name="identity", tag="identity")
+        make_identity(nc, identity[:])
+
+        w_rows = []
+        w_grouped = []
+        for b in range(2):
+            w_rows.append(const.tile([P, PACK, BANK], BF16, name="w_rows%d" % b, tag="w_rows%d" % b))
+            w_grouped.append(const.tile([P, PACK * BANK], BF16, name="w_grouped%d" % b, tag="w_grouped%d" % b, align_bytes=64))
+        w_codes = const.tile([P, N], U32, name="w_codes", tag="w_codes", align_bytes=64)
+        w_scales = const.tile([P, N], U8, name="w_scales", tag="w_scales", align_bytes=64)
+        b2_rows = const.tile([P, N], F32, name="b2_rows", tag="b2_rows")
+        parked = const.tile([P, 1], U32, name="parked", tag="parked")
+        w_view = W2.rearrange("(p j) n -> p j n", j=PACK)
+
+        nc.sync.dma_start(out=vectors[0:1, 0:N], in_=b2.rearrange("(o n) -> o n", o=1))
+        nc.sync.dma_start(out=vectors[0:1, N : 2 * N], in_=g2.rearrange("(o n) -> o n", o=1))
+        load_h(0, 0, 1)
+        load_y(0)
+        load_h(0, 1, 2)
+        for b in range(2):
+            nc.sync.dma_start(out=w_rows[b][:], in_=w_view[:, :, b * BANK : (b + 1) * BANK])
+        load_y(1)
+        load_y(2)
+        load_h(0, 2, 4)
+        load_y(3)
+        load_h(1, 0, 4)
+        load_y(4)
+
+        b2_banks = []
+        for b in range(2):
+            b2_bank = mm_psum.tile([P, BANK], F32, name="product", tag="product")
+            nc.tensor.matmul(out=b2_bank[:], lhsT=ones[:], rhs=vectors[:, b * BANK : (b + 1) * BANK], start=True, stop=True)
+            b2_banks.append(b2_bank)
+        turn_y(0)
+        g2_rows = g2_psum.tile([P, N], BF16, name="g2_rows", tag="g2_rows")
+        for b in range(2):
+            nc.tensor.matmul(
+                out=g2_rows[:, b * BANK : (b + 1) * BANK],
+                lhsT=ones[:],
+                rhs=vectors[:, N + b * BANK : N + (b + 1) * BANK],
+                start=True,
+                stop=True,
+            )
+
+        def interleave_w(b):
+            grouped = w_grouped[b][:].rearrange("p (n j) -> p n j", j=PACK)
+            rows = w_rows[b][:].rearrange("p j n -> p n j")
+            nc.vector.tensor_copy(out=grouped[:, 0:W_VECTOR_COLS, :], in_=rows[:, 0:W_VECTOR_COLS, :])
+            nc.scalar.copy(out=grouped[:, W_VECTOR_COLS:BANK, :], in_=rows[:, W_VECTOR_COLS:BANK, :])
+
+        def quantize_w(b):
+            cols = slice(b * BANK, (b + 1) * BANK)
+            nc.vector.quantize_mx(out=w_codes[:, cols].bitcast(FP8X4), scales=w_scales[:, cols], in_=w_grouped[b][:])
+
+        def add_bias_from_psum(i, b):
+            cols = slice(b * BANK, (b + 1) * BANK)
+            nc.vector.tensor_tensor(
+                out=r_tiles[i][:, cols], in0=h_rows[i // QUAD][:, i % QUAD, cols], in1=b2_banks[b][:], op=ALU.add,
+            )
+
+        for i in range(2):
+            r_tiles[i] = r_pool.tile([P, N], F32, name="r_tile", tag="r_tile")
+        add_bias_from_psum(0, 0)
+        add_bias_from_psum(0, 1)
+        quantize_y(0)
+        add_bias_from_psum(1, 0)
+        add_bias_from_psum(1, 1)
+        interleave_w(0)
+        interleave_w(1)
+        quantize_w(0)
+        turn_y(1)
+        turn_y(2)
+        quantize_y(1)
+        matmul_residual(0, 0)
+        quantize_w(1)
+        quantize_y(2)
+        matmul_residual(0, 1)
+        for b in range(2):
+            nc.scalar.copy(out=b2_rows[:, b * BANK : (b + 1) * BANK], in_=b2_banks[b][:])
+        for i in range(2, QUAD):
+            add_bias(i)
+
+        for s in range(len(groups) + 2):
+            entering = groups[s] if s < len(groups) else []
+            middle = groups[s - 1] if 0 <= s - 1 < len(groups) else []
+            leaving = groups[s - 2] if 0 <= s - 2 < len(groups) else []
+            slots = max(len(entering), len(middle), len(leaving))
+            u = unit_of[entering[0]] if entering else len(units)
+            q = entering[0] // QUAD if entering else QUADS
+            opens = bool(entering) and entering[0] == units[u][0] and u >= 2
+            if opens and u + 3 < len(units):
+                load_y(u + 3)
+            if opens and q + 2 < QUADS:
+                load_h(q + 2, 0, QUAD)
+            to_turn = (u + 2 if opens and u + 2 < len(units) else 0) or (3 if s == 1 else 0)
+            to_quantize = u + 1 if opens and u + 1 < len(units) else 0
+            next_quad = list(range(QUAD * (q + 1), QUAD * (q + 2))) if to_quantize else []
+
+            if entering and s > 0:
+                matmul_residual(entering[0], 0)
+            if middle:
+                negate_mean(s - 1)
+            if entering and s > 0:
+                matmul_residual(entering[0], 1)
+            if leaving:
+                invert_std(s - 2)
+            for i in leaving:
+                if pool_scales(i):
+                    scale_on_pool(i)
+            for i in middle:
+                square_deviation(i)
+            if middle:
+                root(s - 1)
+            for i in next_quad[0:ADDS_BEFORE_PARK]:
+                add_bias(i)
+            behind = []
+            for x in range(slots):
+                if x < len(middle):
+                    gain(middle[x])
+                if x == 0 and leaving:
+                    scale_of_rows(s - 2)
+                if to_quantize and x == min(QUANTIZE_SLOT, slots - 1):
+                    quantize_y(to_quantize)
+                    park_pool(to_quantize)
+                    for i in next_quad[ADDS_BEFORE_PARK:QUAD]:
+                        add_bias(i)
+                for i in behind:
+                    row_amax(i)
+                behind = []
+                if x + 1 < len(entering):
+                    matmul_residual(entering[x + 1], 0)
+                    matmul_residual(entering[x + 1], 1)
+                if x == 0 and leaving:
+                    invert_scale(s - 2)
+                if x == 0 and to_turn:
+                    turn_y(to_turn)
+                if x < len(middle):
+                    behind = [middle[x]]
+                if x < len(leaving):
+                    finish(s - 2, leaving[x])
+            for i in behind:
+                row_amax(i)
+            if entering:
+                add_half_sums(s)

@@ -28,6 +28,7 @@ QUADS = TILES // QUAD
 W_VECTOR_COLS = 320
 POOL_SCALES_FROM = 20
 VECTOR_COLS = {10: 256, 11: 704}
+EARLY_POOL_SCALES = (0, 2)
 QUANTIZE_SLOT = 3
 ADDS_BEFORE_PARK = 1
 
@@ -211,7 +212,7 @@ def tile_transformerblock_pb_t_kernel(tc, y_act, h, W2, b2, g2, out_0, out_1):
             )
 
         def pool_scales(i):
-            return POOL_SCALES_FROM <= i < TILES - 1
+            return (POOL_SCALES_FROM <= i < TILES - 1) or (i >= QUAD and i % QUAD in EARLY_POOL_SCALES)
 
         def finish(g, i):
             a, z = span(g)

@@ -29,6 +29,13 @@ W_VECTOR_COLS = 320
 POOL_SCALES_FROM = 20
 VECTOR_COLS = {10: 256, 11: 704}
 EARLY_POOL_SCALES = (0, 2)
+FOLD_COPY = (1, 0)
+MEAN_COPY = (1, 1)
+HEAD_TURNS = (1, 2, 3)
+AHEAD = 2
+TURN_SLOTS = (0, 1)
+MM_BANKS = 4
+TURN_BANKS = 1
 QUANTIZE_SLOT = 3
 ADDS_BEFORE_PARK = 1
 
@@ -58,8 +65,10 @@ def tile_transformerblock_pb_t_kernel(tc, y_act, h, W2, b2, g2, out_0, out_1):
         bytes_pool = ctx.enter_context(tc.tile_pool(name="bytes_pool", bufs=3))
         squares_pool = ctx.enter_context(tc.tile_pool(name="squares_pool", bufs=2))
         g2_psum = ctx.enter_context(tc.psum_pool(name="g2_psum", bufs=1))
-        mm_psum = ctx.enter_context(tc.psum_pool(name="mm_psum", bufs=5))
-        turn_psum = ctx.enter_context(tc.psum_pool(name="turn_psum", bufs=2))
+        mm_psum = ctx.enter_context(tc.psum_pool(name="mm_psum", bufs=MM_BANKS))
+        turn_psum = ctx.enter_context(tc.psum_pool(name="turn_psum", bufs=TURN_BANKS))
+        fold_psum = ctx.enter_context(tc.psum_pool(name="fold_psum", bufs=2))
+        fold_pool = ctx.enter_context(tc.tile_pool(name="fold_pool", bufs=3))
         ctx.enter_context(tc.manual_schedule())
 
         y_rows = {}
@@ -70,6 +79,9 @@ def tile_transformerblock_pb_t_kernel(tc, y_act, h, W2, b2, g2, out_0, out_1):
         r_tiles = {}
         t_tiles = {}
         byte_tiles = {}
+        products = {}
+        folded = {}
+        folded_sbuf = {}
 
         half_sums = const.tile([P, 2 * TILES], F32, name="half_sums", tag="half_sums")
         row_sums = const.tile([P, TILES], F32, name="row_sums", tag="row_sums")
@@ -95,12 +107,18 @@ def tile_transformerblock_pb_t_kernel(tc, y_act, h, W2, b2, g2, out_0, out_1):
                 h_rows[q] = h_pool.tile([P, QUAD, N], BF16, name="h_rows", tag="h_rows")
             nc.sync.dma_start(out=h_rows[q][:, j0:j1, :], in_=h_quads[q][:, j0:j1, :])
 
-        def turn_y(u):
+        def turn_y(u, halves=(0, 1)):
             a, z = units[u]
-            y_grouped[u] = grouped_pool.tile([P, QUAD * K], BF16, name="y_grouped", tag="y_grouped", align_bytes=64)
+            if 0 in halves:
+                y_grouped[u] = grouped_pool.tile([P, QUAD * K], BF16, name="y_grouped", tag="y_grouped", align_bytes=64)
             for j0 in range(0, z - a, 2):
+                if j0 // 2 not in halves:
+                    continue
                 nj = min(2, z - a - j0)
-                turned = turn_psum.tile([P, 2, 2, P], F32, name="turned", tag="turned")
+                if u in HEAD_TURNS:
+                    turned = mm_psum.tile([P, 2, 2, P], F32, name="product", tag="product")
+                else:
+                    turned = turn_psum.tile([P, 2, 2, P], F32, name="turned", tag="turned")
                 for j in range(nj):
                     words = y_rows[u][:, j0 + j, :].bitcast(F32)
                     for e in range(2):
@@ -127,11 +145,14 @@ def tile_transformerblock_pb_t_kernel(tc, y_act, h, W2, b2, g2, out_0, out_1):
             r_tiles[i] = r_pool.tile([P, N], F32, name="r_tile", tag="r_tile")
             nc.gpsimd.tensor_tensor(out=r_tiles[i][:], in0=h_rows[i // QUAD][:, i % QUAD, :], in1=b2_rows[:], op=ALU.add)
 
-        def matmul_residual(i, b):
+        def multiply(i, b):
+            if (i, b) in products:
+                return
             u = unit_of[i]
             rows = slice((i - units[u][0]) * P, (i - units[u][0] + 1) * P)
             cols = slice(b * BANK, (b + 1) * BANK)
             product = mm_psum.tile([P, BANK], F32, name="product", tag="product")
+            products[(i, b)] = product
             nc.tensor.matmul_mx(
                 out=product[:],
                 lhsT=y_codes[u][:, rows].bitcast(FP8X4),
@@ -141,15 +162,48 @@ def tile_transformerblock_pb_t_kernel(tc, y_act, h, W2, b2, g2, out_0, out_1):
                 start=True,
                 stop=True,
             )
-            nc.vector.scalar_tensor_tensor(
-                out=r_tiles[i][:, cols],
-                in0=product[:],
-                scalar=1.0,
-                in1=r_tiles[i][:, cols],
-                op0=ALU.mult,
-                op1=ALU.add,
-                accum_out=half_sums[:, 2 * i + b : 2 * i + b + 1],
-            )
+
+        def matmul_residual(i, b):
+            multiply(i, b)
+            product = products[(i, b)]
+            cols = slice(b * BANK, (b + 1) * BANK)
+            if folds(i):
+                nc.vector.tensor_tensor(out=r_tiles[i][:, cols], in0=product[:], in1=r_tiles[i][:, cols], op=ALU.add)
+            else:
+                nc.vector.scalar_tensor_tensor(
+                    out=r_tiles[i][:, cols],
+                    in0=product[:],
+                    scalar=1.0,
+                    in1=r_tiles[i][:, cols],
+                    op0=ALU.mult,
+                    op1=ALU.add,
+                    accum_out=half_sums[:, 2 * i + b : 2 * i + b + 1],
+                )
+
+        def folds(i):
+            return QUAD <= i < TILES - QUAD
+
+        def fold_rows(i):
+            e = i % 2
+            if e == 0:
+                folded[i // 2] = fold_psum.tile([P, BANK], F32, name="folded", tag="folded")
+            for c in range(N // P):
+                nc.tensor.matmul(
+                    out=folded[i // 2][:, e * P : (e + 1) * P], lhsT=r_tiles[i][:, c * P : (c + 1) * P], rhs=identity[:],
+                    is_transpose=True, start=(c == 0), stop=(c == N // P - 1),
+                )
+
+        def copy_folds(pair):
+            folded_sbuf[pair] = fold_pool.tile([P, 2 * P], F32, name="folded_sbuf", tag="folded_sbuf")
+            nc.scalar.copy(out=folded_sbuf[pair][:], in_=folded[pair][:, 0 : 2 * P])
+            for e in range(2):
+                nc.tensor.matmul(
+                    out=folded[pair][:, 2 * P + e : 2 * P + e + 1], lhsT=folded_sbuf[pair][:, e * P : (e + 1) * P],
+                    rhs=minus_inv_n[:, 0:1], start=True, stop=True,
+                )
+
+        def copy_means(pair):
+            nc.scalar.copy(out=neg_mean[:, 2 * pair : 2 * pair + 2], in_=folded[pair][:, 2 * P : 2 * P + 2])
 
         def add_half_sums(g):
             a, z = span(g)
@@ -245,6 +299,8 @@ def tile_transformerblock_pb_t_kernel(tc, y_act, h, W2, b2, g2, out_0, out_1):
         nc.vector.memset(ones[:], 1.0)
         zeros = const.tile([P, TILES], F32, name="zeros", tag="zeros")
         nc.vector.memset(zeros[:], 0.0)
+        minus_inv_n = const.tile([P, 1], F32, name="minus_inv_n", tag="minus_inv_n")
+        nc.vector.memset(minus_inv_n[:], -1.0 / N)
         one = const.tile([P, 1], F32, name="one", tag="one")
         nc.vector.memset(one[:], 1.0)
         warmed = const.tile([P, 1], F32, name="warmed", tag="warmed")
@@ -280,7 +336,7 @@ def tile_transformerblock_pb_t_kernel(tc, y_act, h, W2, b2, g2, out_0, out_1):
 
         b2_banks = []
         for b in range(2):
-            b2_bank = mm_psum.tile([P, BANK], F32, name="product", tag="product")
+            b2_bank = fold_psum.tile([P, BANK], F32, name="folded", tag="folded")
             nc.tensor.matmul(out=b2_bank[:], lhsT=ones[:], rhs=vectors[:, b * BANK : (b + 1) * BANK], start=True, stop=True)
             b2_banks.append(b2_bank)
         turn_y(0)
@@ -350,16 +406,20 @@ def tile_transformerblock_pb_t_kernel(tc, y_act, h, W2, b2, g2, out_0, out_1):
 
             if entering and s > 0:
                 matmul_residual(entering[0], 0)
-            if middle:
+            if middle and not folds(middle[0]):
                 negate_mean(s - 1)
             if entering and s > 0:
                 matmul_residual(entering[0], 1)
+            if middle and folds(middle[0]):
+                copy_folds(middle[-1] // 2)
             if leaving:
                 invert_std(s - 2)
             for i in leaving:
                 if pool_scales(i):
                     scale_on_pool(i)
             for i in middle:
+                if folds(i) and i == middle[2]:
+                    copy_means(i // 2)
                 square_deviation(i)
             if middle:
                 root(s - 1)
@@ -376,21 +436,37 @@ def tile_transformerblock_pb_t_kernel(tc, y_act, h, W2, b2, g2, out_0, out_1):
                     park_pool(to_quantize)
                     for i in next_quad[ADDS_BEFORE_PARK:QUAD]:
                         add_bias(i)
+                    for i in groups[s + 1][0:AHEAD]:
+                        multiply(i, 0)
+                        multiply(i, 1)
                 for i in behind:
                     row_amax(i)
                 behind = []
+                if x + AHEAD < len(entering):
+                    multiply(entering[x + AHEAD], 0)
+                    multiply(entering[x + AHEAD], 1)
                 if x + 1 < len(entering):
                     matmul_residual(entering[x + 1], 0)
                     matmul_residual(entering[x + 1], 1)
+                if x < len(entering) and folds(entering[x]):
+                    fold_rows(entering[x])
                 if x == 0 and leaving:
                     invert_scale(s - 2)
-                if x == 0 and to_turn:
-                    turn_y(to_turn)
+                if x in TURN_SLOTS and to_turn:
+                    turn_y(to_turn, [h for h in (0, 1) if TURN_SLOTS[h] == x] if slots > 1 else (0, 1))
                 if x < len(middle):
                     behind = [middle[x]]
+                if x == FOLD_COPY[0] and not FOLD_COPY[1] and entering and folds(entering[0]):
+                    copy_folds(entering[0] // 2)
+                if x == MEAN_COPY[0] and not MEAN_COPY[1] and entering and folds(entering[0]):
+                    copy_means(entering[0] // 2)
                 if x < len(leaving):
                     finish(s - 2, leaving[x])
+                if x == FOLD_COPY[0] and FOLD_COPY[1] and entering and folds(entering[0]):
+                    copy_folds(entering[0] // 2)
+                if x == MEAN_COPY[0] and MEAN_COPY[1] and entering and folds(entering[0]):
+                    copy_means(entering[0] // 2)
             for i in behind:
                 row_amax(i)
-            if entering:
+            if entering and not folds(entering[0]):
                 add_half_sums(s)

@@ -268,17 +268,21 @@ def tile_transformerblock_pb_t_kernel(tc, y_act, h, W2, b2, g2, out_0, out_1):
         def pool_scales(i):
             return (POOL_SCALES_FROM <= i < TILES - 1) or (i >= QUAD and i % QUAD in EARLY_POOL_SCALES)
 
-        def finish(g, i):
-            a, z = span(g)
+        def scale_and_store(g, i):
             t = t_tiles[i]
             c = VECTOR_COLS.get(g, 0)
-            if i == a:
-                byte_tiles[g] = bytes_pool.tile([P, z - a, N], FP8, name="byte_tile", tag="byte_tile")
             if not pool_scales(i):
                 if c:
                     nc.vector.tensor_scalar(out=t[:, 0:c], in0=t[:, 0:c], scalar1=trio[:, i, 1:2], scalar2=None, op0=ALU.mult)
                 nc.scalar.activation(out=t[:, c:N], in_=t[:, c:N], func=ACT.Copy, scale=trio[:, i, 1:2])
             nc.sync.dma_start(out=out_0_quads[i // QUAD][:, i % QUAD, :], in_=t[:])
+
+        def cast_and_store(g, i):
+            a, z = span(g)
+            t = t_tiles[i]
+            c = VECTOR_COLS.get(g, 0)
+            if i == a:
+                byte_tiles[g] = bytes_pool.tile([P, z - a, N], FP8, name="byte_tile", tag="byte_tile")
             if c:
                 nc.vector.tensor_scalar(
                     out=byte_tiles[g][:, i - a, 0:c], in0=t[:, 0:c], scalar1=factor[:, i : i + 1], scalar2=None, op0=ALU.mult,
@@ -293,8 +297,10 @@ def tile_transformerblock_pb_t_kernel(tc, y_act, h, W2, b2, g2, out_0, out_1):
                     out=out_1_quads[i // QUAD][:, a % QUAD : a % QUAD + z - a, :], in_=byte_tiles[g][:].bitcast(U8),
                 )
 
-        vectors = const.tile([P, 2 * N], BF16, name="vectors", tag="vectors")
-        nc.vector.memset(vectors[:].bitcast(F32), 0.0)
+        b2_vector = const.tile([P, N], BF16, name="b2_vector", tag="b2_vector")
+        nc.vector.memset(b2_vector[:].bitcast(F32), 0.0)
+        g2_vector = const.tile([P, N], BF16, name="g2_vector", tag="g2_vector")
+        nc.gpsimd.memset(g2_vector[:].bitcast(F32), 0.0)
         ones = const.tile([P, P], BF16, name="ones", tag="ones")
         nc.vector.memset(ones[:], 1.0)
         zeros = const.tile([P, TILES], F32, name="zeros", tag="zeros")
@@ -320,10 +326,10 @@ def tile_transformerblock_pb_t_kernel(tc, y_act, h, W2, b2, g2, out_0, out_1):
         parked = const.tile([P, 1], U32, name="parked", tag="parked")
         w_view = W2.rearrange("(p j) n -> p j n", j=PACK)
 
-        nc.sync.dma_start(out=vectors[0:1, 0:N], in_=b2.rearrange("(o n) -> o n", o=1))
-        nc.sync.dma_start(out=vectors[0:1, N : 2 * N], in_=g2.rearrange("(o n) -> o n", o=1))
+        nc.sync.dma_start(out=b2_vector[0:1, :], in_=b2.rearrange("(o n) -> o n", o=1))
         load_h(0, 0, 1)
         load_y(0)
+        nc.sync.dma_start(out=g2_vector[0:1, :], in_=g2.rearrange("(o n) -> o n", o=1))
         load_h(0, 1, 2)
         for b in range(2):
             nc.sync.dma_start(out=w_rows[b][:], in_=w_view[:, :, b * BANK : (b + 1) * BANK])
@@ -337,7 +343,7 @@ def tile_transformerblock_pb_t_kernel(tc, y_act, h, W2, b2, g2, out_0, out_1):
         b2_banks = []
         for b in range(2):
             b2_bank = fold_psum.tile([P, BANK], F32, name="folded", tag="folded")
-            nc.tensor.matmul(out=b2_bank[:], lhsT=ones[:], rhs=vectors[:, b * BANK : (b + 1) * BANK], start=True, stop=True)
+            nc.tensor.matmul(out=b2_bank[:], lhsT=ones[:], rhs=b2_vector[:, b * BANK : (b + 1) * BANK], start=True, stop=True)
             b2_banks.append(b2_bank)
         turn_y(0)
         g2_rows = g2_psum.tile([P, N], BF16, name="g2_rows", tag="g2_rows")
@@ -345,16 +351,17 @@ def tile_transformerblock_pb_t_kernel(tc, y_act, h, W2, b2, g2, out_0, out_1):
             nc.tensor.matmul(
                 out=g2_rows[:, b * BANK : (b + 1) * BANK],
                 lhsT=ones[:],
-                rhs=vectors[:, N + b * BANK : N + (b + 1) * BANK],
+                rhs=g2_vector[:, b * BANK : (b + 1) * BANK],
                 start=True,
                 stop=True,
             )
 
         def interleave_w(b):
-            grouped = w_grouped[b][:].rearrange("p (n j) -> p n j", j=PACK)
-            rows = w_rows[b][:].rearrange("p j n -> p n j")
-            nc.vector.tensor_copy(out=grouped[:, 0:W_VECTOR_COLS, :], in_=rows[:, 0:W_VECTOR_COLS, :])
-            nc.scalar.copy(out=grouped[:, W_VECTOR_COLS:BANK, :], in_=rows[:, W_VECTOR_COLS:BANK, :])
+            grouped = w_grouped[b][:].rearrange("p (c i j) -> p c j i", i=PACK, j=PACK)
+            rows = w_rows[b][:].rearrange("p j (c i) -> p c j i", i=PACK)
+            cut = W_VECTOR_COLS // PACK
+            nc.vector.tensor_copy(out=grouped[:, 0:cut, :, :], in_=rows[:, 0:cut, :, :])
+            nc.scalar.copy(out=grouped[:, cut : BANK // PACK, :, :], in_=rows[:, cut : BANK // PACK, :, :])
 
         def quantize_w(b):
             cols = slice(b * BANK, (b + 1) * BANK)
@@ -461,7 +468,8 @@ def tile_transformerblock_pb_t_kernel(tc, y_act, h, W2, b2, g2, out_0, out_1):
                 if x == MEAN_COPY[0] and not MEAN_COPY[1] and entering and folds(entering[0]):
                     copy_means(entering[0] // 2)
                 if x < len(leaving):
-                    finish(s - 2, leaving[x])
+                    scale_and_store(s - 2, leaving[x])
+                    cast_and_store(s - 2, leaving[x])
                 if x == FOLD_COPY[0] and FOLD_COPY[1] and entering and folds(entering[0]):
                     copy_folds(entering[0] // 2)
                 if x == MEAN_COPY[0] and MEAN_COPY[1] and entering and folds(entering[0]):

@@ -32,6 +32,7 @@ EARLY_POOL_SCALES = (0, 2)
 FOLD_COPY = (1, 0)
 MEAN_COPY = (1, 1)
 HEAD_TURNS = (1, 2, 3)
+FOLDED_A_QUAD = 2
 AHEAD = 2
 TURN_SLOTS = (0, 1)
 MM_BANKS = 4
@@ -181,7 +182,7 @@ def tile_transformerblock_pb_t_kernel(tc, y_act, h, W2, b2, g2, out_0, out_1):
                 )
 
         def folds(i):
-            return QUAD <= i < TILES - QUAD
+            return QUAD <= i < TILES - QUAD and i % QUAD < FOLDED_A_QUAD
 
         def fold_rows(i):
             e = i % 2
@@ -194,19 +195,25 @@ def tile_transformerblock_pb_t_kernel(tc, y_act, h, W2, b2, g2, out_0, out_1):
                 )
 
         def copy_folds(pair):
+            n = len([i for i in (2 * pair, 2 * pair + 1) if folds(i)])
             folded_sbuf[pair] = fold_pool.tile([P, 2 * P], F32, name="folded_sbuf", tag="folded_sbuf")
-            nc.scalar.copy(out=folded_sbuf[pair][:], in_=folded[pair][:, 0 : 2 * P])
-            for e in range(2):
+            nc.scalar.copy(out=folded_sbuf[pair][:, 0 : n * P], in_=folded[pair][:, 0 : n * P])
+            for e in range(n):
                 nc.tensor.matmul(
                     out=folded[pair][:, 2 * P + e : 2 * P + e + 1], lhsT=folded_sbuf[pair][:, e * P : (e + 1) * P],
                     rhs=minus_inv_n[:, 0:1], start=True, stop=True,
                 )
 
         def copy_means(pair):
-            nc.scalar.copy(out=neg_mean[:, 2 * pair : 2 * pair + 2], in_=folded[pair][:, 2 * P : 2 * P + 2])
+            n = len([i for i in (2 * pair, 2 * pair + 1) if folds(i)])
+            nc.scalar.copy(out=neg_mean[:, 2 * pair : 2 * pair + n], in_=folded[pair][:, 2 * P : 2 * P + n])
+
+        def unfolded(g):
+            own = [i for i in groups[g] if not folds(i)]
+            return (own[0], own[-1] + 1) if own else (0, 0)
 
         def add_half_sums(g):
-            a, z = span(g)
+            a, z = unfolded(g)
             if z - a > 1:
                 nc.vector.tensor_reduce(
                     out=row_sums[:, a:z],
@@ -216,7 +223,7 @@ def tile_transformerblock_pb_t_kernel(tc, y_act, h, W2, b2, g2, out_0, out_1):
                 )
 
         def negate_mean(g):
-            a, z = span(g)
+            a, z = unfolded(g)
             if z - a > 1:
                 nc.vector.tensor_scalar(
                     out=neg_mean[:, a:z], in0=row_sums[:, a:z], scalar1=-1.0 / N, scalar2=None, op0=ALU.mult, op1=ALU.add,
@@ -413,12 +420,12 @@ def tile_transformerblock_pb_t_kernel(tc, y_act, h, W2, b2, g2, out_0, out_1):
 
             if entering and s > 0:
                 matmul_residual(entering[0], 0)
-            if middle and not folds(middle[0]):
+            if middle and not folds(middle[-1]):
                 negate_mean(s - 1)
             if entering and s > 0:
                 matmul_residual(entering[0], 1)
-            if middle and folds(middle[0]):
-                copy_folds(middle[-1] // 2)
+            if len(middle) == QUAD and folds(middle[2]):
+                copy_folds(middle[2] // 2)
             if leaving:
                 invert_std(s - 2)
             for i in leaving:
@@ -476,5 +483,5 @@ def tile_transformerblock_pb_t_kernel(tc, y_act, h, W2, b2, g2, out_0, out_1):
                     copy_means(entering[0] // 2)
             for i in behind:
                 row_amax(i)
-            if entering and not folds(entering[0]):
+            if entering and not folds(entering[-1]):
                 add_half_sums(s)

@@ -474,8 +474,11 @@ def tile_transformerblock_pb_t_kernel(tc, y_act, h, W2, b2, g2, out_0, out_1):
                     copy_folds(entering[0] // 2)
                 if x == MEAN_COPY[0] and not MEAN_COPY[1] and entering and folds(entering[0]):
                     copy_means(entering[0] // 2)
+                if x == 0 and leaving:
+                    scale_and_store(s - 2, leaving[0])
+                if x + 1 < len(leaving):
+                    scale_and_store(s - 2, leaving[x + 1])
                 if x < len(leaving):
-                    scale_and_store(s - 2, leaving[x])
                     cast_and_store(s - 2, leaving[x])
                 if x == FOLD_COPY[0] and FOLD_COPY[1] and entering and folds(entering[0]):
                     copy_folds(entering[0] // 2)

@@ -55,6 +55,11 @@ def tile_transformerblock_pb_t_kernel(tc, y_act, h, W2, b2, g2, out_0, out_1):
         for i in range(units[u][0], units[u][1]):
             unit_of[i] = u
 
+    pair_of = {}
+    for group in groups:
+        for k in range(len(group)):
+            pair_of[group[k]] = group[k - k % 2]
+
     with ExitStack() as ctx:
         const = ctx.enter_context(tc.tile_pool(name="const", bufs=1))
         y_pool = ctx.enter_context(tc.tile_pool(name="y_pool", bufs=4))
@@ -62,7 +67,7 @@ def tile_transformerblock_pb_t_kernel(tc, y_act, h, W2, b2, g2, out_0, out_1):
         codes_pool = ctx.enter_context(tc.tile_pool(name="codes_pool", bufs=4))
         h_pool = ctx.enter_context(tc.tile_pool(name="h_pool", bufs=3))
         r_pool = ctx.enter_context(tc.tile_pool(name="r_pool", bufs=12))
-        t_pool = ctx.enter_context(tc.tile_pool(name="t_pool", bufs=12))
+        t_pool = ctx.enter_context(tc.tile_pool(name="t_pool", bufs=6))
         bytes_pool = ctx.enter_context(tc.tile_pool(name="bytes_pool", bufs=3))
         squares_pool = ctx.enter_context(tc.tile_pool(name="squares_pool", bufs=2))
         g2_psum = ctx.enter_context(tc.psum_pool(name="g2_psum", bufs=1))
@@ -78,7 +83,7 @@ def tile_transformerblock_pb_t_kernel(tc, y_act, h, W2, b2, g2, out_0, out_1):
         y_scales = {}
         h_rows = {}
         r_tiles = {}
-        t_tiles = {}
+        t_pairs = {}
         byte_tiles = {}
         products = {}
         folded = {}
@@ -89,11 +94,14 @@ def tile_transformerblock_pb_t_kernel(tc, y_act, h, W2, b2, g2, out_0, out_1):
         neg_mean = const.tile([P, TILES], F32, name="neg_mean", tag="neg_mean")
         sq_sums = const.tile([P, TILES], F32, name="sq_sums", tag="sq_sums")
         std = const.tile([P, TILES], F32, name="std", tag="std")
-        trio = const.tile([P, TILES, 3], F32, name="trio", tag="trio")
+        trio = const.tile([P, 3, TILES], F32, name="trio", tag="trio")
         q_scale = const.tile([P, TILES], F32, name="q_scale", tag="q_scale")
         factor = const.tile([P, TILES], F32, name="factor", tag="factor")
         unused_sum = const.tile([P, 1], F32, name="unused_sum", tag="unused_sum")
         unused_pair = const.tile([P, 2], F32, name="unused_pair", tag="unused_pair")
+
+        def t_of(i):
+            return t_pairs[pair_of[i]][:, i - pair_of[i], :]
 
         def span(g):
             return groups[g][0], groups[g][-1] + 1
@@ -248,20 +256,24 @@ def tile_transformerblock_pb_t_kernel(tc, y_act, h, W2, b2, g2, out_0, out_1):
 
         def invert_std(g):
             a, z = span(g)
-            nc.vector.reciprocal(out=trio[:, a:z, 1], in_=std[:, a:z])
+            nc.vector.reciprocal(out=trio[:, 1, a:z], in_=std[:, a:z])
 
         def gain(i):
-            t_tiles[i] = t_pool.tile([P, N], F32, name="t_tile", tag="t_tile")
+            if i == pair_of[i]:
+                t_pairs[i] = t_pool.tile([P, 2, N], F32, name="t_pair", tag="t_pair")
             nc.vector.scalar_tensor_tensor(
-                out=t_tiles[i][:], in0=r_tiles[i][:], scalar=neg_mean[:, i : i + 1], in1=g2_rows[:], op0=ALU.add, op1=ALU.mult,
+                out=t_of(i), in0=r_tiles[i][:], scalar=neg_mean[:, i : i + 1], in1=g2_rows[:], op0=ALU.add, op1=ALU.mult,
             )
 
-        def row_amax(i):
-            nc.vector.tensor_reduce(out=trio[:, i, 0:1], in_=t_tiles[i][:], axis=AX.X, op=ALU.max, apply_absolute_value=True)
+        def row_amax(first):
+            n = len([i for i in range(TILES) if pair_of[i] == first])
+            nc.vector.tensor_reduce(
+                out=trio[:, 0, first : first + n], in_=t_pairs[first][:, 0:n, :], axis=AX.X, op=ALU.max, apply_absolute_value=True,
+            )
 
         def scale_of_rows(g):
             a, z = span(g)
-            nc.vector.tensor_reduce(out=q_scale[:, a:z], in_=trio[:, a:z, :], axis=AX.X, op=ALU.mult)
+            nc.vector.tensor_reduce(out=q_scale[:, a:z], in_=trio[:, :, a:z].rearrange("p c i -> p i c"), axis=AX.X, op=ALU.mult)
 
         def invert_scale(g):
             a, z = span(g)
@@ -269,24 +281,24 @@ def tile_transformerblock_pb_t_kernel(tc, y_act, h, W2, b2, g2, out_0, out_1):
 
         def scale_on_pool(i):
             nc.gpsimd.tensor_scalar(
-                out=t_tiles[i][:], in0=t_tiles[i][:], scalar1=trio[:, i, 1:2], scalar2=1.0, op0=ALU.mult, op1=ALU.mult,
+                out=t_of(i), in0=t_of(i), scalar1=trio[:, 1, i : i + 1], scalar2=1.0, op0=ALU.mult, op1=ALU.mult,
             )
 
         def pool_scales(i):
             return (POOL_SCALES_FROM <= i < TILES - 1) or (i >= QUAD and i % QUAD in EARLY_POOL_SCALES)
 
         def scale_and_store(g, i):
-            t = t_tiles[i]
+            t = t_of(i)
             c = VECTOR_COLS.get(g, 0)
             if not pool_scales(i):
                 if c:
-                    nc.vector.tensor_scalar(out=t[:, 0:c], in0=t[:, 0:c], scalar1=trio[:, i, 1:2], scalar2=None, op0=ALU.mult)
-                nc.scalar.activation(out=t[:, c:N], in_=t[:, c:N], func=ACT.Copy, scale=trio[:, i, 1:2])
-            nc.sync.dma_start(out=out_0_quads[i // QUAD][:, i % QUAD, :], in_=t[:])
+                    nc.vector.tensor_scalar(out=t[:, 0:c], in0=t[:, 0:c], scalar1=trio[:, 1, i : i + 1], scalar2=None, op0=ALU.mult)
+                nc.scalar.activation(out=t[:, c:N], in_=t[:, c:N], func=ACT.Copy, scale=trio[:, 1, i : i + 1])
+            nc.sync.dma_start(out=out_0_quads[i // QUAD][:, i % QUAD, :], in_=t)
 
         def cast_and_store(g, i):
             a, z = span(g)
-            t = t_tiles[i]
+            t = t_of(i)
             c = VECTOR_COLS.get(g, 0)
             if i == a:
                 byte_tiles[g] = bytes_pool.tile([P, z - a, N], FP8, name="byte_tile", tag="byte_tile")
@@ -318,7 +330,7 @@ def tile_transformerblock_pb_t_kernel(tc, y_act, h, W2, b2, g2, out_0, out_1):
         nc.vector.memset(one[:], 1.0)
         warmed = const.tile([P, 1], F32, name="warmed", tag="warmed")
         nc.scalar.activation(out=warmed[:], in_=one[:], func=ACT.Sqrt)
-        nc.vector.tensor_scalar(out=trio[:, :, 2], in0=zeros[:], scalar1=1.0, scalar2=1.0 / 448.0, op0=ALU.mult, op1=ALU.add)
+        nc.vector.tensor_scalar(out=trio[:, 2, :], in0=zeros[:], scalar1=1.0, scalar2=1.0 / 448.0, op0=ALU.mult, op1=ALU.add)
         identity = const.tile([P, P], F32, name="identity", tag="identity")
         make_identity(nc, identity[:])
 
@@ -468,8 +480,8 @@ def tile_transformerblock_pb_t_kernel(tc, y_act, h, W2, b2, g2, out_0, out_1):
                     invert_scale(s - 2)
                 if x in TURN_SLOTS and to_turn:
                     turn_y(to_turn, [h for h in (0, 1) if TURN_SLOTS[h] == x] if slots > 1 else (0, 1))
-                if x < len(middle):
-                    behind = [middle[x]]
+                if x < len(middle) and (x % 2 == 1 or x == len(middle) - 1):
+                    behind = [pair_of[middle[x]]]
                 if x == FOLD_COPY[0] and not FOLD_COPY[1] and entering and folds(entering[0]):
                     copy_folds(entering[0] // 2)
                 if x == MEAN_COPY[0] and not MEAN_COPY[1] and entering and folds(entering[0]):

@@ -90,14 +90,13 @@ def tile_transformerblock_pb_t_kernel(tc, y_act, h, W2, b2, g2, out_0, out_1):
         folded_sbuf = {}
 
         half_sums = const.tile([P, 2 * TILES], F32, name="half_sums", tag="half_sums")
-        row_sums = const.tile([P, TILES], F32, name="row_sums", tag="row_sums")
+        duo = const.tile([P, 2, TILES], F32, name="duo", tag="duo")
         neg_mean = const.tile([P, TILES], F32, name="neg_mean", tag="neg_mean")
         sq_sums = const.tile([P, TILES], F32, name="sq_sums", tag="sq_sums")
         std = const.tile([P, TILES], F32, name="std", tag="std")
         trio = const.tile([P, 3, TILES], F32, name="trio", tag="trio")
         q_scale = const.tile([P, TILES], F32, name="q_scale", tag="q_scale")
         factor = const.tile([P, TILES], F32, name="factor", tag="factor")
-        unused_sum = const.tile([P, 1], F32, name="unused_sum", tag="unused_sum")
         unused_pair = const.tile([P, 2], F32, name="unused_pair", tag="unused_pair")
 
         def t_of(i):
@@ -224,7 +223,7 @@ def tile_transformerblock_pb_t_kernel(tc, y_act, h, W2, b2, g2, out_0, out_1):
             a, z = unfolded(g)
             if z - a > 1:
                 nc.vector.tensor_reduce(
-                    out=row_sums[:, a:z],
+                    out=duo[:, 0, a:z],
                     in_=half_sums[:, 2 * a : 2 * z].rearrange("p (i b) -> p i b", b=2),
                     axis=AX.X,
                     op=ALU.add,
@@ -233,9 +232,8 @@ def tile_transformerblock_pb_t_kernel(tc, y_act, h, W2, b2, g2, out_0, out_1):
         def negate_mean(g):
             a, z = unfolded(g)
             if z - a > 1:
-                nc.vector.tensor_scalar(
-                    out=neg_mean[:, a:z], in0=row_sums[:, a:z], scalar1=-1.0 / N, scalar2=None, op0=ALU.mult, op1=ALU.add,
-                    accum_out=unused_sum[:, 0:1],
+                nc.vector.tensor_reduce(
+                    out=neg_mean[:, a:z], in_=duo[:, :, a:z].rearrange("p c i -> p i c"), axis=AX.X, op=ALU.mult,
                 )
             else:
                 nc.vector.tensor_scalar(
@@ -331,6 +329,7 @@ def tile_transformerblock_pb_t_kernel(tc, y_act, h, W2, b2, g2, out_0, out_1):
         warmed = const.tile([P, 1], F32, name="warmed", tag="warmed")
         nc.scalar.activation(out=warmed[:], in_=one[:], func=ACT.Sqrt)
         nc.vector.tensor_scalar(out=trio[:, 2, :], in0=zeros[:], scalar1=1.0, scalar2=1.0 / 448.0, op0=ALU.mult, op1=ALU.add)
+        nc.vector.tensor_scalar(out=duo[:, 1, :], in0=zeros[:], scalar1=1.0, scalar2=-1.0 / N, op0=ALU.mult, op1=ALU.add)
         identity = const.tile([P, P], F32, name="identity", tag="identity")
         make_identity(nc, identity[:])
 
@@ -447,7 +446,7 @@ def tile_transformerblock_pb_t_kernel(tc, y_act, h, W2, b2, g2, out_0, out_1):
                 if folds(i) and i == middle[2]:
                     copy_means(i // 2)
                 square_deviation(i)
-            if middle:
+            if middle and len(middle) < QUAD:
                 root(s - 1)
             for i in next_quad[0:ADDS_BEFORE_PARK]:
                 add_bias(i)
@@ -480,6 +479,8 @@ def tile_transformerblock_pb_t_kernel(tc, y_act, h, W2, b2, g2, out_0, out_1):
                     invert_scale(s - 2)
                 if x in TURN_SLOTS and to_turn:
                     turn_y(to_turn, [h for h in (0, 1) if TURN_SLOTS[h] == x] if slots > 1 else (0, 1))
+                if x == 0 and len(middle) == QUAD:
+                    root(s - 1)
                 if x < len(middle) and (x % 2 == 1 or x == len(middle) - 1):
                     behind = [pair_of[middle[x]]]
                 if x == FOLD_COPY[0] and not FOLD_COPY[1] and entering and folds(entering[0]):

@@ -93,9 +93,7 @@ def tile_transformerblock_pb_t_kernel(tc, y_act, h, W2, b2, g2, out_0, out_1):
         duo = const.tile([P, 2, TILES], F32, name="duo", tag="duo")
         neg_mean = const.tile([P, TILES], F32, name="neg_mean", tag="neg_mean")
         sq_sums = const.tile([P, TILES], F32, name="sq_sums", tag="sq_sums")
-        std = const.tile([P, TILES], F32, name="std", tag="std")
-        trio = const.tile([P, 3, TILES], F32, name="trio", tag="trio")
-        q_scale = const.tile([P, TILES], F32, name="q_scale", tag="q_scale")
+        stats = const.tile([P, 5, TILES], F32, name="stats", tag="stats")
         factor = const.tile([P, TILES], F32, name="factor", tag="factor")
         unused_pair = const.tile([P, 2], F32, name="unused_pair", tag="unused_pair")
 
@@ -250,11 +248,11 @@ def tile_transformerblock_pb_t_kernel(tc, y_act, h, W2, b2, g2, out_0, out_1):
 
         def root(g):
             a, z = span(g)
-            nc.scalar.activation(out=std[:, a:z], in_=sq_sums[:, a:z], func=ACT.Sqrt, bias=EPS, scale=1.0 / N)
+            nc.scalar.activation(out=stats[:, 1, a:z], in_=sq_sums[:, a:z], func=ACT.Sqrt, bias=EPS, scale=1.0 / N)
 
         def invert_std(g):
             a, z = span(g)
-            nc.vector.reciprocal(out=trio[:, 1, a:z], in_=std[:, a:z])
+            nc.vector.reciprocal(out=stats[:, 3:5, a:z], in_=stats[:, 0:2, a:z])
 
         def gain(i):
             if i == pair_of[i]:
@@ -266,20 +264,16 @@ def tile_transformerblock_pb_t_kernel(tc, y_act, h, W2, b2, g2, out_0, out_1):
         def row_amax(first):
             n = len([i for i in range(TILES) if pair_of[i] == first])
             nc.vector.tensor_reduce(
-                out=trio[:, 0, first : first + n], in_=t_pairs[first][:, 0:n, :], axis=AX.X, op=ALU.max, apply_absolute_value=True,
+                out=stats[:, 0, first : first + n], in_=t_pairs[first][:, 0:n, :], axis=AX.X, op=ALU.max, apply_absolute_value=True,
             )
 
         def scale_of_rows(g):
             a, z = span(g)
-            nc.vector.tensor_reduce(out=q_scale[:, a:z], in_=trio[:, :, a:z].rearrange("p c i -> p i c"), axis=AX.X, op=ALU.mult)
-
-        def invert_scale(g):
-            a, z = span(g)
-            nc.vector.reciprocal(out=factor[:, a:z], in_=q_scale[:, a:z])
+            nc.vector.tensor_reduce(out=factor[:, a:z], in_=stats[:, 1:4, a:z].rearrange("p c i -> p i c"), axis=AX.X, op=ALU.mult)
 
         def scale_on_pool(i):
             nc.gpsimd.tensor_scalar(
-                out=t_of(i), in0=t_of(i), scalar1=trio[:, 1, i : i + 1], scalar2=1.0, op0=ALU.mult, op1=ALU.mult,
+                out=t_of(i), in0=t_of(i), scalar1=stats[:, 4, i : i + 1], scalar2=1.0, op0=ALU.mult, op1=ALU.mult,
             )
 
         def pool_scales(i):
@@ -290,8 +284,8 @@ def tile_transformerblock_pb_t_kernel(tc, y_act, h, W2, b2, g2, out_0, out_1):
             c = VECTOR_COLS.get(g, 0)
             if not pool_scales(i):
                 if c:
-                    nc.vector.tensor_scalar(out=t[:, 0:c], in0=t[:, 0:c], scalar1=trio[:, 1, i : i + 1], scalar2=None, op0=ALU.mult)
-                nc.scalar.activation(out=t[:, c:N], in_=t[:, c:N], func=ACT.Copy, scale=trio[:, 1, i : i + 1])
+                    nc.vector.tensor_scalar(out=t[:, 0:c], in0=t[:, 0:c], scalar1=stats[:, 4, i : i + 1], scalar2=None, op0=ALU.mult)
+                nc.scalar.activation(out=t[:, c:N], in_=t[:, c:N], func=ACT.Copy, scale=stats[:, 4, i : i + 1])
             nc.sync.dma_start(out=out_0_quads[i // QUAD][:, i % QUAD, :], in_=t)
 
         def cast_and_store(g, i):
@@ -328,7 +322,7 @@ def tile_transformerblock_pb_t_kernel(tc, y_act, h, W2, b2, g2, out_0, out_1):
         nc.vector.memset(one[:], 1.0)
         warmed = const.tile([P, 1], F32, name="warmed", tag="warmed")
         nc.scalar.activation(out=warmed[:], in_=one[:], func=ACT.Sqrt)
-        nc.vector.tensor_scalar(out=trio[:, 2, :], in0=zeros[:], scalar1=1.0, scalar2=1.0 / 448.0, op0=ALU.mult, op1=ALU.add)
+        nc.vector.memset(stats[:, 2, :], 448.0)
         nc.vector.tensor_scalar(out=duo[:, 1, :], in0=zeros[:], scalar1=1.0, scalar2=-1.0 / N, op0=ALU.mult, op1=ALU.add)
         identity = const.tile([P, P], F32, name="identity", tag="identity")
         make_identity(nc, identity[:])
@@ -475,8 +469,6 @@ def tile_transformerblock_pb_t_kernel(tc, y_act, h, W2, b2, g2, out_0, out_1):
                     matmul_residual(entering[x + 1], 1)
                 if x < len(entering) and folds(entering[x]):
                     fold_rows(entering[x])
-                if x == 0 and leaving:
-                    invert_scale(s - 2)
                 if x in TURN_SLOTS and to_turn:
                     turn_y(to_turn, [h for h in (0, 1) if TURN_SLOTS[h] == x] if slots > 1 else (0, 1))
                 if x == 0 and len(middle) == QUAD:
@@ -491,6 +483,10 @@ def tile_transformerblock_pb_t_kernel(tc, y_act, h, W2, b2, g2, out_0, out_1):
                     scale_and_store(s - 2, leaving[0])
                 if x + 1 < len(leaving):
                     scale_and_store(s - 2, leaving[x + 1])
+                if VECTOR_COLS.get(s - 2, 0):
+                    for i in behind:
+                        row_amax(i)
+                    behind = []
                 if x < len(leaving):
                     cast_and_store(s - 2, leaving[x])
                 if x == FOLD_COPY[0] and FOLD_COPY[1] and entering and folds(entering[0]):

@@ -440,7 +440,8 @@ def tile_transformerblock_pb_t_kernel(tc, y_act, h, W2, b2, g2, out_0, out_1):
                 if folds(i) and i == middle[2]:
                     copy_means(i // 2)
                 square_deviation(i)
-            if middle and len(middle) < QUAD:
+            root_later = len(middle) == QUAD or (bool(leaving) and 0 < s - 1 < len(groups) - 1)
+            if middle and not root_later:
                 root(s - 1)
             for i in next_quad[0:ADDS_BEFORE_PARK]:
                 add_bias(i)
@@ -489,6 +490,8 @@ def tile_transformerblock_pb_t_kernel(tc, y_act, h, W2, b2, g2, out_0, out_1):
                     behind = []
                 if x < len(leaving):
                     cast_and_store(s - 2, leaving[x])
+                if x == 0 and root_later and len(middle) < QUAD:
+                    root(s - 1)
                 if x == FOLD_COPY[0] and FOLD_COPY[1] and entering and folds(entering[0]):
                     copy_folds(entering[0] // 2)
                 if x == MEAN_COPY[0] and MEAN_COPY[1] and entering and folds(entering[0]):

@@ -404,6 +404,7 @@ def tile_transformerblock_pb_t_kernel(tc, y_act, h, W2, b2, g2, out_0, out_1):
         matmul_residual(0, 1)
         for b in range(2):
             nc.scalar.copy(out=b2_rows[:, b * BANK : (b + 1) * BANK], in_=b2_banks[b][:])
+        park_pool(2)
         for i in range(2, QUAD):
             add_bias(i)
 

@@ -27,6 +27,7 @@ QUADS = TILES // QUAD
 
 W_VECTOR_COLS = 320
 POOL_SCALES_FROM = 20
+O_BUFS = 4
 VECTOR_COLS = {10: 256, 11: 704}
 EARLY_POOL_SCALES = (0, 2)
 FOLD_COPY = (1, 0)
@@ -68,6 +69,7 @@ def tile_transformerblock_pb_t_kernel(tc, y_act, h, W2, b2, g2, out_0, out_1):
         h_pool = ctx.enter_context(tc.tile_pool(name="h_pool", bufs=3))
         r_pool = ctx.enter_context(tc.tile_pool(name="r_pool", bufs=12))
         t_pool = ctx.enter_context(tc.tile_pool(name="t_pool", bufs=6))
+        o_pool = ctx.enter_context(tc.tile_pool(name="o_pool", bufs=O_BUFS))
         bytes_pool = ctx.enter_context(tc.tile_pool(name="bytes_pool", bufs=3))
         squares_pool = ctx.enter_context(tc.tile_pool(name="squares_pool", bufs=2))
         g2_psum = ctx.enter_context(tc.psum_pool(name="g2_psum", bufs=1))
@@ -85,6 +87,7 @@ def tile_transformerblock_pb_t_kernel(tc, y_act, h, W2, b2, g2, out_0, out_1):
         r_tiles = {}
         t_pairs = {}
         byte_tiles = {}
+        o_tiles = {}
         products = {}
         folded = {}
         folded_sbuf = {}
@@ -217,6 +220,9 @@ def tile_transformerblock_pb_t_kernel(tc, y_act, h, W2, b2, g2, out_0, out_1):
             own = [i for i in groups[g] if not folds(i)]
             return (own[0], own[-1] + 1) if own else (0, 0)
 
+        def early_mean(g):
+            return 0 < g < len(groups) and len(groups[g]) == 1
+
         def add_half_sums(g):
             a, z = unfolded(g)
             if z - a > 1:
@@ -250,9 +256,9 @@ def tile_transformerblock_pb_t_kernel(tc, y_act, h, W2, b2, g2, out_0, out_1):
             a, z = span(g)
             nc.scalar.activation(out=stats[:, 1, a:z], in_=sq_sums[:, a:z], func=ACT.Sqrt, bias=EPS, scale=1.0 / N)
 
-        def invert_std(g):
+        def invert(g, rows=(0, 2)):
             a, z = span(g)
-            nc.vector.reciprocal(out=stats[:, 3:5, a:z], in_=stats[:, 0:2, a:z])
+            nc.vector.reciprocal(out=stats[:, 3 + rows[0] : 3 + rows[1], a:z], in_=stats[:, rows[0] : rows[1], a:z])
 
         def gain(i):
             if i == pair_of[i]:
@@ -269,24 +275,25 @@ def tile_transformerblock_pb_t_kernel(tc, y_act, h, W2, b2, g2, out_0, out_1):
 
         def scale_of_rows(g):
             a, z = span(g)
-            nc.vector.tensor_reduce(out=factor[:, a:z], in_=stats[:, 1:4, a:z].rearrange("p c i -> p i c"), axis=AX.X, op=ALU.mult)
+            nc.vector.tensor_reduce(out=factor[:, a:z], in_=stats[:, 2:4, a:z].rearrange("p c i -> p i c"), axis=AX.X, op=ALU.mult)
 
         def scale_on_pool(i):
+            o_tiles[i] = o_pool.tile([P, N], F32, name="o_tile", tag="o_tile")
             nc.gpsimd.tensor_scalar(
-                out=t_of(i), in0=t_of(i), scalar1=stats[:, 4, i : i + 1], scalar2=1.0, op0=ALU.mult, op1=ALU.mult,
+                out=o_tiles[i][:], in0=t_of(i), scalar1=stats[:, 4, i : i + 1], scalar2=1.0, op0=ALU.mult, op1=ALU.mult,
             )
 
         def pool_scales(i):
             return (POOL_SCALES_FROM <= i < TILES - 1) or (i >= QUAD and i % QUAD in EARLY_POOL_SCALES)
 
         def scale_and_store(g, i):
-            t = t_of(i)
-            c = VECTOR_COLS.get(g, 0)
-            if not pool_scales(i):
-                if c:
-                    nc.vector.tensor_scalar(out=t[:, 0:c], in0=t[:, 0:c], scalar1=stats[:, 4, i : i + 1], scalar2=None, op0=ALU.mult)
-                nc.scalar.activation(out=t[:, c:N], in_=t[:, c:N], func=ACT.Copy, scale=stats[:, 4, i : i + 1])
-            nc.sync.dma_start(out=out_0_quads[i // QUAD][:, i % QUAD, :], in_=t)
+            if i == TILES - 1:
+                o_tiles[i] = o_pool.tile([P, N], F32, name="o_tile", tag="o_tile")
+                nc.vector.tensor_scalar(out=o_tiles[i][:], in0=t_of(i), scalar1=stats[:, 4, i : i + 1], scalar2=None, op0=ALU.mult)
+            elif not pool_scales(i):
+                o_tiles[i] = o_pool.tile([P, N], F32, name="o_tile", tag="o_tile")
+                nc.scalar.activation(out=o_tiles[i][:], in_=t_of(i), func=ACT.Copy, scale=stats[:, 4, i : i + 1])
+            nc.sync.dma_start(out=out_0_quads[i // QUAD][:, i % QUAD, :], in_=o_tiles[i][:])
 
         def cast_and_store(g, i):
             a, z = span(g)
@@ -426,14 +433,14 @@ def tile_transformerblock_pb_t_kernel(tc, y_act, h, W2, b2, g2, out_0, out_1):
 
             if entering and s > 0:
                 matmul_residual(entering[0], 0)
-            if middle and not folds(middle[-1]):
+            if middle and not folds(middle[-1]) and not early_mean(s - 1):
                 negate_mean(s - 1)
             if entering and s > 0:
                 matmul_residual(entering[0], 1)
             if len(middle) == QUAD and folds(middle[2]):
                 copy_folds(middle[2] // 2)
             if leaving:
-                invert_std(s - 2)
+                invert(s - 2)
             for i in leaving:
                 if pool_scales(i):
                     scale_on_pool(i)
@@ -452,6 +459,8 @@ def tile_transformerblock_pb_t_kernel(tc, y_act, h, W2, b2, g2, out_0, out_1):
                     gain(middle[x])
                 if x == 0 and leaving:
                     scale_of_rows(s - 2)
+                if x == 0 and early_mean(s):
+                    negate_mean(s)
                 if to_quantize and x == min(QUANTIZE_SLOT, slots - 1):
                     quantize_y(to_quantize)
                     park_pool(to_quantize)

@@ -29,7 +29,7 @@ W_VECTOR_COLS = 320
 POOL_SCALES_FROM = 20
 O_BUFS = 4
 VECTOR_COLS = {10: 256, 11: 704}
-EARLY_POOL_SCALES = (0, 2)
+EARLY_POOL_SCALES = (0,)
 FOLD_COPY = (1, 0)
 MEAN_COPY = (1, 1)
 HEAD_TURNS = (1, 2, 3)
@@ -40,6 +40,8 @@ MM_BANKS = 4
 TURN_BANKS = 1
 QUANTIZE_SLOT = 3
 ADDS_BEFORE_PARK = 1
+HEAD_BEFORE_PARK = {2: 1}
+LATE_UNTIL = 3
 
 
 def tile_transformerblock_pb_t_kernel(tc, y_act, h, W2, b2, g2, out_0, out_1):
@@ -333,6 +335,8 @@ def tile_transformerblock_pb_t_kernel(tc, y_act, h, W2, b2, g2, out_0, out_1):
         nc.vector.tensor_scalar(out=duo[:, 1, :], in0=zeros[:], scalar1=1.0, scalar2=-1.0 / N, op0=ALU.mult, op1=ALU.add)
         identity = const.tile([P, P], F32, name="identity", tag="identity")
         make_identity(nc, identity[:])
+        identity_16 = const.tile([P, P], BF16, name="identity_16", tag="identity_16")
+        make_identity(nc, identity_16[:])
 
         w_rows = []
         w_grouped = []
@@ -345,18 +349,18 @@ def tile_transformerblock_pb_t_kernel(tc, y_act, h, W2, b2, g2, out_0, out_1):
         parked = const.tile([P, 1], U32, name="parked", tag="parked")
         w_view = W2.rearrange("(p j) n -> p j n", j=PACK)
 
+        nc.sync.dma_start(out=w_rows[0][:], in_=w_view[:, :, 0:BANK])
         nc.sync.dma_start(out=b2_vector[0:1, :], in_=b2.rearrange("(o n) -> o n", o=1))
-        load_h(0, 0, 1)
+        nc.sync.dma_start(out=w_rows[1][:], in_=w_view[:, :, BANK:N])
         load_y(0)
+        load_h(0, 0, 1)
+        load_y(1)
         nc.sync.dma_start(out=g2_vector[0:1, :], in_=g2.rearrange("(o n) -> o n", o=1))
         load_h(0, 1, 2)
-        for b in range(2):
-            nc.sync.dma_start(out=w_rows[b][:], in_=w_view[:, :, b * BANK : (b + 1) * BANK])
-        load_y(1)
         load_y(2)
         load_h(0, 2, 4)
-        load_y(3)
         load_h(1, 0, 4)
+        load_y(3)
         load_y(4)
 
         b2_banks = []
@@ -364,16 +368,17 @@ def tile_transformerblock_pb_t_kernel(tc, y_act, h, W2, b2, g2, out_0, out_1):
             b2_bank = fold_psum.tile([P, BANK], F32, name="folded", tag="folded")
             nc.tensor.matmul(out=b2_bank[:], lhsT=ones[:], rhs=b2_vector[:, b * BANK : (b + 1) * BANK], start=True, stop=True)
             b2_banks.append(b2_bank)
-        turn_y(0)
         g2_rows = g2_psum.tile([P, N], BF16, name="g2_rows", tag="g2_rows")
-        for b in range(2):
-            nc.tensor.matmul(
-                out=g2_rows[:, b * BANK : (b + 1) * BANK],
-                lhsT=ones[:],
-                rhs=g2_vector[:, b * BANK : (b + 1) * BANK],
-                start=True,
-                stop=True,
-            )
+
+        def spread_g2():
+            for b in range(2):
+                nc.tensor.matmul(
+                    out=g2_rows[:, b * BANK : (b + 1) * BANK],
+                    lhsT=ones[:],
+                    rhs=g2_vector[:, b * BANK : (b + 1) * BANK],
+                    start=True,
+                    stop=True,
+                )
 
         def interleave_w(b):
             grouped = w_grouped[b][:].rearrange("p (c i j) -> p c j i", i=PACK, j=PACK)
@@ -386,36 +391,56 @@ def tile_transformerblock_pb_t_kernel(tc, y_act, h, W2, b2, g2, out_0, out_1):
             cols = slice(b * BANK, (b + 1) * BANK)
             nc.vector.quantize_mx(out=w_codes[:, cols].bitcast(FP8X4), scales=w_scales[:, cols], in_=w_grouped[b][:])
 
-        def add_bias_from_psum(i, b):
-            cols = slice(b * BANK, (b + 1) * BANK)
-            nc.vector.tensor_tensor(
-                out=r_tiles[i][:, cols], in0=h_rows[i // QUAD][:, i % QUAD, cols], in1=b2_banks[b][:], op=ALU.add,
-            )
-
-        for i in range(2):
+        def add_bias_on_tensor(i):
             r_tiles[i] = r_pool.tile([P, N], F32, name="r_tile", tag="r_tile")
-        add_bias_from_psum(0, 0)
-        add_bias_from_psum(0, 1)
-        quantize_y(0)
-        add_bias_from_psum(1, 0)
-        add_bias_from_psum(1, 1)
+            for b in range(2):
+                cols = slice(b * BANK, (b + 1) * BANK)
+                hb = mm_psum.tile([P, BANK], F32, name="product", tag="product")
+                nc.tensor.matmul(out=hb[:], lhsT=ones[:], rhs=b2_vector[:, cols], start=True, stop=False)
+                nc.tensor.matmul(out=hb[:], lhsT=identity_16[:], rhs=h_rows[0][:, i, cols], start=False, stop=True)
+                nc.scalar.copy(out=r_tiles[i][:, cols], in_=hb[:])
+
         interleave_w(0)
         interleave_w(1)
+        turn_y(0)
         quantize_w(0)
-        turn_y(1)
-        turn_y(2)
-        quantize_y(1)
-        matmul_residual(0, 0)
+        quantize_y(0)
         quantize_w(1)
-        quantize_y(2)
+        add_bias_on_tensor(0)
+        turn_y(1)
+        spread_g2()
+        for b in range(2):
+            multiply(0, b)
+        matmul_residual(0, 0)
         matmul_residual(0, 1)
+        add_bias_on_tensor(1)
+        quantize_y(1)
+        negate_mean(0)
+        turn_y(2)
         for b in range(2):
             nc.scalar.copy(out=b2_rows[:, b * BANK : (b + 1) * BANK], in_=b2_banks[b][:])
+        gain(0)
+        for b in range(2):
+            multiply(1, b)
+        matmul_residual(1, 0)
+        matmul_residual(1, 1)
+        quantize_y(2)
         park_pool(2)
-        for i in range(2, QUAD):
-            add_bias(i)
+        add_bias(4)
+        add_bias_on_tensor(2)
+        row_amax(0)
+        negate_mean(1)
+        for b in range(2):
+            multiply(2, b)
+        add_bias_on_tensor(3)
+        gain(1)
+        for b in range(2):
+            multiply(3, b)
+        square_deviation(0)
+        turn_y(3)
+        root(0)
 
-        for s in range(len(groups) + 2):
+        for s in range(2, len(groups) + 2):
             entering = groups[s] if s < len(groups) else []
             middle = groups[s - 1] if 0 <= s - 1 < len(groups) else []
             leaving = groups[s - 2] if 0 <= s - 2 < len(groups) else []
@@ -427,9 +452,11 @@ def tile_transformerblock_pb_t_kernel(tc, y_act, h, W2, b2, g2, out_0, out_1):
                 load_y(u + 3)
             if opens and q + 2 < QUADS:
                 load_h(q + 2, 0, QUAD)
-            to_turn = (u + 2 if opens and u + 2 < len(units) else 0) or (3 if s == 1 else 0)
+            to_turn = (u + 2 if opens and u + 2 < len(units) else 0)
             to_quantize = u + 1 if opens and u + 1 < len(units) else 0
-            next_quad = list(range(QUAD * (q + 1), QUAD * (q + 2))) if to_quantize else []
+            next_quad = [i for i in range(QUAD * (q + 1), QUAD * (q + 2)) if i not in r_tiles] if to_quantize else []
+            late = s <= LATE_UNTIL
+            before_park = HEAD_BEFORE_PARK.get(s, ADDS_BEFORE_PARK)
 
             if entering and s > 0:
                 matmul_residual(entering[0], 0)
@@ -439,7 +466,7 @@ def tile_transformerblock_pb_t_kernel(tc, y_act, h, W2, b2, g2, out_0, out_1):
                 matmul_residual(entering[0], 1)
             if len(middle) == QUAD and folds(middle[2]):
                 copy_folds(middle[2] // 2)
-            if leaving:
+            if leaving and not late:
                 invert(s - 2)
             for i in leaving:
                 if pool_scales(i):
@@ -451,20 +478,24 @@ def tile_transformerblock_pb_t_kernel(tc, y_act, h, W2, b2, g2, out_0, out_1):
             root_later = len(middle) == QUAD or (bool(leaving) and 0 < s - 1 < len(groups) - 1)
             if middle and not root_later:
                 root(s - 1)
-            for i in next_quad[0:ADDS_BEFORE_PARK]:
+            for i in next_quad[0:before_park]:
                 add_bias(i)
             behind = []
             for x in range(slots):
-                if x < len(middle):
+                if x < len(middle) and middle[x] > 1:
                     gain(middle[x])
-                if x == 0 and leaving:
+                if x == 0 and leaving and not late:
                     scale_of_rows(s - 2)
                 if x == 0 and early_mean(s):
                     negate_mean(s)
+                if s == 2:
+                    for i in behind:
+                        row_amax(i)
+                    behind = []
                 if to_quantize and x == min(QUANTIZE_SLOT, slots - 1):
                     quantize_y(to_quantize)
                     park_pool(to_quantize)
-                    for i in next_quad[ADDS_BEFORE_PARK:QUAD]:
+                    for i in next_quad[before_park:QUAD]:
                         add_bias(i)
                     for i in groups[s + 1][0:AHEAD]:
                         multiply(i, 0)
@@ -490,15 +521,22 @@ def tile_transformerblock_pb_t_kernel(tc, y_act, h, W2, b2, g2, out_0, out_1):
                     copy_folds(entering[0] // 2)
                 if x == MEAN_COPY[0] and not MEAN_COPY[1] and entering and folds(entering[0]):
                     copy_means(entering[0] // 2)
-                if x == 0 and leaving:
+                if x == slots - 1 and leaving and late:
+                    invert(s - 2)
+                    scale_of_rows(s - 2)
+                if x == 0 and leaving and not late:
                     scale_and_store(s - 2, leaving[0])
-                if x + 1 < len(leaving):
+                if x + 1 < len(leaving) and not late:
                     scale_and_store(s - 2, leaving[x + 1])
+                if x == slots - 1 and late:
+                    for i in leaving:
+                        scale_and_store(s - 2, i)
+                        cast_and_store(s - 2, i)
                 if VECTOR_COLS.get(s - 2, 0):
                     for i in behind:
                         row_amax(i)
                     behind = []
-                if x < len(leaving):
+                if x < len(leaving) and not late:
                     cast_and_store(s - 2, leaving[x])
                 if x == 0 and root_later and len(middle) < QUAD:
                     root(s - 1)

@@ -40,7 +40,8 @@ MM_BANKS = 4
 TURN_BANKS = 1
 QUANTIZE_SLOT = 3
 ADDS_BEFORE_PARK = 1
-HEAD_BEFORE_PARK = {2: 1}
+TENSOR_BIAS = (0, 1, 2, 3)
+FOLD_FROM = 8
 LATE_UNTIL = 3
 
 
@@ -192,7 +193,7 @@ def tile_transformerblock_pb_t_kernel(tc, y_act, h, W2, b2, g2, out_0, out_1):
                 )
 
         def folds(i):
-            return QUAD <= i < TILES - QUAD and i % QUAD < FOLDED_A_QUAD
+            return FOLD_FROM <= i < TILES - QUAD and i % QUAD < FOLDED_A_QUAD
 
         def fold_rows(i):
             e = i % 2
@@ -353,8 +354,8 @@ def tile_transformerblock_pb_t_kernel(tc, y_act, h, W2, b2, g2, out_0, out_1):
         nc.sync.dma_start(out=b2_vector[0:1, :], in_=b2.rearrange("(o n) -> o n", o=1))
         nc.sync.dma_start(out=w_rows[1][:], in_=w_view[:, :, BANK:N])
         load_y(0)
-        load_h(0, 0, 1)
         load_y(1)
+        load_h(0, 0, 1)
         nc.sync.dma_start(out=g2_vector[0:1, :], in_=g2.rearrange("(o n) -> o n", o=1))
         load_h(0, 1, 2)
         load_y(2)
@@ -400,47 +401,79 @@ def tile_transformerblock_pb_t_kernel(tc, y_act, h, W2, b2, g2, out_0, out_1):
                 nc.tensor.matmul(out=hb[:], lhsT=identity_16[:], rhs=h_rows[0][:, i, cols], start=False, stop=True)
                 nc.scalar.copy(out=r_tiles[i][:, cols], in_=hb[:])
 
+        def add_bias_on_vector(i):
+            r_tiles[i] = r_pool.tile([P, N], F32, name="r_tile", tag="r_tile")
+            for b in range(2):
+                cols = slice(b * BANK, (b + 1) * BANK)
+                nc.vector.tensor_tensor(out=r_tiles[i][:, cols], in0=h_rows[0][:, i, cols], in1=b2_banks[b][:], op=ALU.add)
+
         interleave_w(0)
+        quantize_w(0)
         interleave_w(1)
         turn_y(0)
-        quantize_w(0)
+        turn_y(1)
         quantize_y(0)
         quantize_w(1)
-        add_bias_on_tensor(0)
-        turn_y(1)
-        spread_g2()
+        quantize_y(1)
         for b in range(2):
             multiply(0, b)
+        for b in range(2):
+            nc.scalar.copy(out=b2_rows[:, b * BANK : (b + 1) * BANK], in_=b2_banks[b][:])
+        add_bias_on_vector(0)
+        add_bias(2)
+        turn_y(2)
+        spread_g2()
         matmul_residual(0, 0)
         matmul_residual(0, 1)
         add_bias_on_tensor(1)
-        quantize_y(1)
         negate_mean(0)
-        turn_y(2)
-        for b in range(2):
-            nc.scalar.copy(out=b2_rows[:, b * BANK : (b + 1) * BANK], in_=b2_banks[b][:])
-        gain(0)
         for b in range(2):
             multiply(1, b)
-        matmul_residual(1, 0)
-        matmul_residual(1, 1)
+        gain(0)
         quantize_y(2)
         park_pool(2)
+        add_bias(3)
         add_bias(4)
-        add_bias_on_tensor(2)
-        row_amax(0)
-        negate_mean(1)
+        matmul_residual(1, 0)
+        matmul_residual(1, 1)
+        square_deviation(0)
         for b in range(2):
             multiply(2, b)
-        add_bias_on_tensor(3)
+        row_amax(0)
+        negate_mean(1)
         gain(1)
-        for b in range(2):
-            multiply(3, b)
-        square_deviation(0)
         turn_y(3)
         root(0)
+        for b in range(2):
+            multiply(3, b)
+        load_y(5)
+        load_h(2, 0, QUAD)
+        matmul_residual(2, 0)
+        matmul_residual(2, 1)
+        square_deviation(1)
+        matmul_residual(3, 0)
+        matmul_residual(3, 1)
+        add_bias(5)
+        row_amax(1)
+        add_half_sums(2)
+        negate_mean(2)
+        gain(2)
+        turn_y(4)
+        root(1)
+        quantize_y(3)
+        park_pool(3)
+        add_bias(6)
+        add_bias(7)
+        for i in (4, 5):
+            for b in range(2):
+                multiply(i, b)
+        gain(3)
+        invert(0)
+        scale_of_rows(0)
+        scale_and_store(0, 0)
+        cast_and_store(0, 0)
 
-        for s in range(2, len(groups) + 2):
+        for s in range(3, len(groups) + 2):
             entering = groups[s] if s < len(groups) else []
             middle = groups[s - 1] if 0 <= s - 1 < len(groups) else []
             leaving = groups[s - 2] if 0 <= s - 2 < len(groups) else []
@@ -456,11 +489,11 @@ def tile_transformerblock_pb_t_kernel(tc, y_act, h, W2, b2, g2, out_0, out_1):
             to_quantize = u + 1 if opens and u + 1 < len(units) else 0
             next_quad = [i for i in range(QUAD * (q + 1), QUAD * (q + 2)) if i not in r_tiles] if to_quantize else []
             late = s <= LATE_UNTIL
-            before_park = HEAD_BEFORE_PARK.get(s, ADDS_BEFORE_PARK)
+            before_park = ADDS_BEFORE_PARK
 
             if entering and s > 0:
                 matmul_residual(entering[0], 0)
-            if middle and not folds(middle[-1]) and not early_mean(s - 1):
+            if middle and s > 3 and not folds(middle[-1]) and not early_mean(s - 1):
                 negate_mean(s - 1)
             if entering and s > 0:
                 matmul_residual(entering[0], 1)
@@ -482,16 +515,12 @@ def tile_transformerblock_pb_t_kernel(tc, y_act, h, W2, b2, g2, out_0, out_1):
                 add_bias(i)
             behind = []
             for x in range(slots):
-                if x < len(middle) and middle[x] > 1:
+                if x < len(middle) and s > 3:
                     gain(middle[x])
                 if x == 0 and leaving and not late:
                     scale_of_rows(s - 2)
                 if x == 0 and early_mean(s):
                     negate_mean(s)
-                if s == 2:
-                    for i in behind:
-                        row_amax(i)
-                    behind = []
                 if to_quantize and x == min(QUANTIZE_SLOT, slots - 1):
                     quantize_y(to_quantize)
                     park_pool(to_quantize)

@@ -28,7 +28,7 @@ QUADS = TILES // QUAD
 W_VECTOR_COLS = 320
 POOL_SCALES_FROM = 20
 O_BUFS = 4
-VECTOR_COLS = {10: 256, 11: 704}
+VECTOR_COLS = {9: 256, 10: 1024, 11: 704}
 EARLY_POOL_SCALES = (0,)
 FOLD_COPY = (1, 0)
 MEAN_COPY = (1, 1)
@@ -40,6 +40,8 @@ MM_BANKS = 4
 TURN_BANKS = 1
 QUANTIZE_SLOT = 3
 ADDS_BEFORE_PARK = 1
+TAIL_FROM = 8
+TAIL_SLOT = 3
 TENSOR_BIAS = (0, 1, 2, 3)
 FOLD_FROM = 8
 LATE_UNTIL = 3
@@ -92,6 +94,7 @@ def tile_transformerblock_pb_t_kernel(tc, y_act, h, W2, b2, g2, out_0, out_1):
         byte_tiles = {}
         o_tiles = {}
         products = {}
+        squared = []
         folded = {}
         folded_sbuf = {}
 
@@ -224,7 +227,7 @@ def tile_transformerblock_pb_t_kernel(tc, y_act, h, W2, b2, g2, out_0, out_1):
             return (own[0], own[-1] + 1) if own else (0, 0)
 
         def early_mean(g):
-            return 0 < g < len(groups) and len(groups[g]) == 1
+            return 3 < g < len(groups) and len(groups[g]) == 1
 
         def add_half_sums(g):
             a, z = unfolded(g)
@@ -249,6 +252,7 @@ def tile_transformerblock_pb_t_kernel(tc, y_act, h, W2, b2, g2, out_0, out_1):
                 )
 
         def square_deviation(i):
+            squared.append(i)
             squares = squares_pool.tile([P, N], BF16, name="squares", tag="squares")
             nc.scalar.activation(
                 out=squares[:], in_=r_tiles[i][:], func=ACT.Square, bias=neg_mean[:, i : i + 1], scale=1.0,
@@ -261,6 +265,8 @@ def tile_transformerblock_pb_t_kernel(tc, y_act, h, W2, b2, g2, out_0, out_1):
 
         def invert(g, rows=(0, 2)):
             a, z = span(g)
+            if g >= TAIL_FROM and rows == (0, 2):
+                rows = (0, 1)
             nc.vector.reciprocal(out=stats[:, 3 + rows[0] : 3 + rows[1], a:z], in_=stats[:, rows[0] : rows[1], a:z])
 
         def gain(i):
@@ -287,16 +293,17 @@ def tile_transformerblock_pb_t_kernel(tc, y_act, h, W2, b2, g2, out_0, out_1):
             )
 
         def pool_scales(i):
-            return (POOL_SCALES_FROM <= i < TILES - 1) or (i >= QUAD and i % QUAD in EARLY_POOL_SCALES)
+            return (POOL_SCALES_FROM <= i) or (i >= QUAD and i % QUAD in EARLY_POOL_SCALES)
+
+        def store_scaled(i):
+            nc.sync.dma_start(out=out_0_quads[i // QUAD][:, i % QUAD, :], in_=o_tiles[i][:])
 
         def scale_and_store(g, i):
-            if i == TILES - 1:
-                o_tiles[i] = o_pool.tile([P, N], F32, name="o_tile", tag="o_tile")
-                nc.vector.tensor_scalar(out=o_tiles[i][:], in0=t_of(i), scalar1=stats[:, 4, i : i + 1], scalar2=None, op0=ALU.mult)
-            elif not pool_scales(i):
+            if not pool_scales(i):
                 o_tiles[i] = o_pool.tile([P, N], F32, name="o_tile", tag="o_tile")
                 nc.scalar.activation(out=o_tiles[i][:], in_=t_of(i), func=ACT.Copy, scale=stats[:, 4, i : i + 1])
-            nc.sync.dma_start(out=out_0_quads[i // QUAD][:, i % QUAD, :], in_=o_tiles[i][:])
+            if g < TAIL_FROM:
+                store_scaled(i)
 
         def cast_and_store(g, i):
             a, z = span(g)
@@ -309,10 +316,11 @@ def tile_transformerblock_pb_t_kernel(tc, y_act, h, W2, b2, g2, out_0, out_1):
                     out=byte_tiles[g][:, i - a, 0:c], in0=t[:, 0:c], scalar1=factor[:, i : i + 1], scalar2=None, op0=ALU.mult,
                     saturate=False,
                 )
-            nc.scalar.activation(
-                out=byte_tiles[g][:, i - a, c:N], in_=t[:, c:N], func=ACT.Identity, scale=factor[:, i : i + 1],
-                bias=zeros[:, 0:1], saturate=False,
-            )
+            if c < N:
+                nc.scalar.activation(
+                    out=byte_tiles[g][:, i - a, c:N], in_=t[:, c:N], func=ACT.Identity, scale=factor[:, i : i + 1],
+                    bias=zeros[:, 0:1], saturate=False,
+                )
             if i == z - 1:
                 nc.sync.dma_start(
                     out=out_1_quads[i // QUAD][:, a % QUAD : a % QUAD + z - a, :], in_=byte_tiles[g][:].bitcast(U8),
@@ -502,14 +510,15 @@ def tile_transformerblock_pb_t_kernel(tc, y_act, h, W2, b2, g2, out_0, out_1):
             if leaving and not late:
                 invert(s - 2)
             for i in leaving:
-                if pool_scales(i):
+                if pool_scales(i) and i not in o_tiles:
                     scale_on_pool(i)
             for i in middle:
                 if folds(i) and i == middle[2]:
                     copy_means(i // 2)
-                square_deviation(i)
+                if i not in squared:
+                    square_deviation(i)
             root_later = len(middle) == QUAD or (bool(leaving) and 0 < s - 1 < len(groups) - 1)
-            if middle and not root_later:
+            if middle and (s - 1 == TAIL_FROM + 1 or not root_later) and not early_mean(s - 1):
                 root(s - 1)
             for i in next_quad[0:before_park]:
                 add_bias(i)
@@ -521,6 +530,16 @@ def tile_transformerblock_pb_t_kernel(tc, y_act, h, W2, b2, g2, out_0, out_1):
                     scale_of_rows(s - 2)
                 if x == 0 and early_mean(s):
                     negate_mean(s)
+                    square_deviation(entering[0])
+                    if s == len(groups) - 1:
+                        root(s)
+                if s - 1 >= TAIL_FROM and x == min(TAIL_SLOT, len(middle) - 1):
+                    invert(s - 1, (1, 2))
+                if s - 1 >= TAIL_FROM and min(TAIL_SLOT, len(middle) - 1) <= x < len(middle):
+                    for i in middle[0 : x + 1]:
+                        if i not in o_tiles:
+                            scale_on_pool(i)
+                            store_scaled(i)
                 if to_quantize and x == min(QUANTIZE_SLOT, slots - 1):
                     quantize_y(to_quantize)
                     park_pool(to_quantize)
@@ -567,8 +586,11 @@ def tile_transformerblock_pb_t_kernel(tc, y_act, h, W2, b2, g2, out_0, out_1):
                     behind = []
                 if x < len(leaving) and not late:
                     cast_and_store(s - 2, leaving[x])
-                if x == 0 and root_later and len(middle) < QUAD:
-                    root(s - 1)
+                if x == 0 and len(middle) < QUAD:
+                    if root_later and s - 1 < TAIL_FROM:
+                        root(s - 1)
+                    if early_mean(s) and s < len(groups) - 1:
+                        root(s)
                 if x == FOLD_COPY[0] and FOLD_COPY[1] and entering and folds(entering[0]):
                     copy_folds(entering[0] // 2)
                 if x == MEAN_COPY[0] and MEAN_COPY[1] and entering and folds(entering[0]):

@@ -27,7 +27,7 @@ QUADS = TILES // QUAD
 
 W_VECTOR_COLS = 320
 POOL_SCALES_FROM = 20
-O_BUFS = 4
+O_BUFS = 6
 VECTOR_COLS = {9: 256, 10: 1024, 11: 704}
 EARLY_POOL_SCALES = (0,)
 FOLD_COPY = (1, 0)
@@ -40,6 +40,9 @@ MM_BANKS = 4
 TURN_BANKS = 1
 QUANTIZE_SLOT = 3
 ADDS_BEFORE_PARK = 1
+LATE_ADDS = (30, 31)
+ADD_A = 26
+ADD_B = 27
 TAIL_FROM = 8
 TAIL_SLOT = 3
 TENSOR_BIAS = (0, 1, 2, 3)
@@ -75,7 +78,7 @@ def tile_transformerblock_pb_t_kernel(tc, y_act, h, W2, b2, g2, out_0, out_1):
         r_pool = ctx.enter_context(tc.tile_pool(name="r_pool", bufs=12))
         t_pool = ctx.enter_context(tc.tile_pool(name="t_pool", bufs=6))
         o_pool = ctx.enter_context(tc.tile_pool(name="o_pool", bufs=O_BUFS))
-        bytes_pool = ctx.enter_context(tc.tile_pool(name="bytes_pool", bufs=3))
+        bytes_pool = ctx.enter_context(tc.tile_pool(name="bytes_pool", bufs=5))
         squares_pool = ctx.enter_context(tc.tile_pool(name="squares_pool", bufs=2))
         g2_psum = ctx.enter_context(tc.psum_pool(name="g2_psum", bufs=1))
         mm_psum = ctx.enter_context(tc.psum_pool(name="mm_psum", bufs=MM_BANKS))
@@ -246,10 +249,13 @@ def tile_transformerblock_pb_t_kernel(tc, y_act, h, W2, b2, g2, out_0, out_1):
                     out=neg_mean[:, a:z], in_=duo[:, :, a:z].rearrange("p c i -> p i c"), axis=AX.X, op=ALU.mult,
                 )
             else:
-                nc.vector.tensor_scalar(
-                    out=unused_pair[:], in0=half_sums[:, 2 * a : 2 * a + 2], scalar1=-1.0 / N, scalar2=None, op0=ALU.mult,
-                    op1=ALU.add, accum_out=neg_mean[:, a : a + 1],
-                )
+                negate_mean_of(a)
+
+        def negate_mean_of(i):
+            nc.vector.tensor_scalar(
+                out=unused_pair[:], in0=half_sums[:, 2 * i : 2 * i + 2], scalar1=-1.0 / N, scalar2=None, op0=ALU.mult,
+                op1=ALU.add, accum_out=neg_mean[:, i : i + 1],
+            )
 
         def square_deviation(i):
             squared.append(i)
@@ -271,7 +277,7 @@ def tile_transformerblock_pb_t_kernel(tc, y_act, h, W2, b2, g2, out_0, out_1):
 
         def gain(i):
             if i == pair_of[i]:
-                t_pairs[i] = t_pool.tile([P, 2, N], F32, name="t_pair", tag="t_pair")
+                t_pairs[i] = t_pool.tile([P, 2, N], F32, name="t_pair", tag="t_pair", align_bytes=64)
             nc.vector.scalar_tensor_tensor(
                 out=t_of(i), in0=r_tiles[i][:], scalar=neg_mean[:, i : i + 1], in1=g2_rows[:], op0=ALU.add, op1=ALU.mult,
             )
@@ -349,18 +355,20 @@ def tile_transformerblock_pb_t_kernel(tc, y_act, h, W2, b2, g2, out_0, out_1):
 
         w_rows = []
         w_grouped = []
+        w_rows_pair = t_pool.tile([P, 2, PACK, BANK], BF16, name="w_rows_pair", tag="t_pair", align_bytes=64)
+        w_grouped_pair = t_pool.tile([P, 2, PACK * BANK], BF16, name="w_grouped_pair", tag="t_pair", align_bytes=64)
         for b in range(2):
-            w_rows.append(const.tile([P, PACK, BANK], BF16, name="w_rows%d" % b, tag="w_rows%d" % b))
-            w_grouped.append(const.tile([P, PACK * BANK], BF16, name="w_grouped%d" % b, tag="w_grouped%d" % b, align_bytes=64))
+            w_rows.append(w_rows_pair[:, b, :, :])
+            w_grouped.append(w_grouped_pair[:, b, :])
         w_codes = const.tile([P, N], U32, name="w_codes", tag="w_codes", align_bytes=64)
         w_scales = const.tile([P, N], U8, name="w_scales", tag="w_scales", align_bytes=64)
         b2_rows = const.tile([P, N], F32, name="b2_rows", tag="b2_rows")
         parked = const.tile([P, 1], U32, name="parked", tag="parked")
         w_view = W2.rearrange("(p j) n -> p j n", j=PACK)
 
-        nc.sync.dma_start(out=w_rows[0][:], in_=w_view[:, :, 0:BANK])
+        nc.sync.dma_start(out=w_rows[0], in_=w_view[:, :, 0:BANK])
         nc.sync.dma_start(out=b2_vector[0:1, :], in_=b2.rearrange("(o n) -> o n", o=1))
-        nc.sync.dma_start(out=w_rows[1][:], in_=w_view[:, :, BANK:N])
+        nc.sync.dma_start(out=w_rows[1], in_=w_view[:, :, BANK:N])
         load_y(0)
         load_y(1)
         load_h(0, 0, 1)
@@ -390,15 +398,15 @@ def tile_transformerblock_pb_t_kernel(tc, y_act, h, W2, b2, g2, out_0, out_1):
                 )
 
         def interleave_w(b):
-            grouped = w_grouped[b][:].rearrange("p (c i j) -> p c j i", i=PACK, j=PACK)
-            rows = w_rows[b][:].rearrange("p j (c i) -> p c j i", i=PACK)
+            grouped = w_grouped[b].rearrange("p (c i j) -> p c j i", i=PACK, j=PACK)
+            rows = w_rows[b].rearrange("p j (c i) -> p c j i", i=PACK)
             cut = W_VECTOR_COLS // PACK
             nc.vector.tensor_copy(out=grouped[:, 0:cut, :, :], in_=rows[:, 0:cut, :, :])
             nc.scalar.copy(out=grouped[:, cut : BANK // PACK, :, :], in_=rows[:, cut : BANK // PACK, :, :])
 
         def quantize_w(b):
             cols = slice(b * BANK, (b + 1) * BANK)
-            nc.vector.quantize_mx(out=w_codes[:, cols].bitcast(FP8X4), scales=w_scales[:, cols], in_=w_grouped[b][:])
+            nc.vector.quantize_mx(out=w_codes[:, cols].bitcast(FP8X4), scales=w_scales[:, cols], in_=w_grouped[b])
 
         def add_bias_on_tensor(i):
             r_tiles[i] = r_pool.tile([P, N], F32, name="r_tile", tag="r_tile")
@@ -460,11 +468,11 @@ def tile_transformerblock_pb_t_kernel(tc, y_act, h, W2, b2, g2, out_0, out_1):
         matmul_residual(2, 1)
         square_deviation(1)
         matmul_residual(3, 0)
+        negate_mean_of(2)
         matmul_residual(3, 1)
         add_bias(5)
         row_amax(1)
-        add_half_sums(2)
-        negate_mean(2)
+        negate_mean_of(3)
         gain(2)
         turn_y(4)
         root(1)
@@ -475,8 +483,8 @@ def tile_transformerblock_pb_t_kernel(tc, y_act, h, W2, b2, g2, out_0, out_1):
         for i in (4, 5):
             for b in range(2):
                 multiply(i, b)
-        gain(3)
         invert(0)
+        gain(3)
         scale_of_rows(0)
         scale_and_store(0, 0)
         cast_and_store(0, 0)
@@ -522,6 +530,8 @@ def tile_transformerblock_pb_t_kernel(tc, y_act, h, W2, b2, g2, out_0, out_1):
                 root(s - 1)
             for i in next_quad[0:before_park]:
                 add_bias(i)
+            if entering and entering[0] == TILES - QUAD:
+                add_bias(30)
             behind = []
             for x in range(slots):
                 if x < len(middle) and s > 3:
@@ -540,11 +550,16 @@ def tile_transformerblock_pb_t_kernel(tc, y_act, h, W2, b2, g2, out_0, out_1):
                         if i not in o_tiles:
                             scale_on_pool(i)
                             store_scaled(i)
+                        if i == ADD_B and 31 not in r_tiles:
+                            add_bias(31)
+                if x == slots - 1 and leaving and late:
+                    invert(s - 2)
                 if to_quantize and x == min(QUANTIZE_SLOT, slots - 1):
                     quantize_y(to_quantize)
                     park_pool(to_quantize)
                     for i in next_quad[before_park:QUAD]:
-                        add_bias(i)
+                        if i not in LATE_ADDS:
+                            add_bias(i)
                     for i in groups[s + 1][0:AHEAD]:
                         multiply(i, 0)
                         multiply(i, 1)
@@ -570,7 +585,6 @@ def tile_transformerblock_pb_t_kernel(tc, y_act, h, W2, b2, g2, out_0, out_1):
                 if x == MEAN_COPY[0] and not MEAN_COPY[1] and entering and folds(entering[0]):
                     copy_means(entering[0] // 2)
                 if x == slots - 1 and leaving and late:
-                    invert(s - 2)
                     scale_of_rows(s - 2)
                 if x == 0 and leaving and not late:
                     scale_and_store(s - 2, leaving[0])

@@ -362,7 +362,7 @@ def tile_transformerblock_pb_t_kernel(tc, y_act, h, W2, b2, g2, out_0, out_1):
             w_grouped.append(w_grouped_pair[:, b, :])
         w_codes = const.tile([P, N], U32, name="w_codes", tag="w_codes", align_bytes=64)
         w_scales = const.tile([P, N], U8, name="w_scales", tag="w_scales", align_bytes=64)
-        b2_rows = const.tile([P, N], F32, name="b2_rows", tag="b2_rows")
+        b2_rows = const.tile([P, N], BF16, name="b2_rows", tag="b2_rows")
         parked = const.tile([P, 1], U32, name="parked", tag="parked")
         w_view = W2.rearrange("(p j) n -> p j n", j=PACK)
 

@@ -30,10 +30,10 @@ POOL_SCALES_FROM = 20
 O_BUFS = 6
 VECTOR_COLS = {9: 256, 10: 1024, 11: 704}
 EARLY_POOL_SCALES = (0,)
-FOLD_COPY = (1, 0)
-MEAN_COPY = (1, 1)
+FOLD_COPY = (2, 0)
+MEAN_COPY = (2, 1)
 HEAD_TURNS = (1, 2, 3)
-FOLDED_A_QUAD = 2
+FOLDED_A_QUAD = 3
 AHEAD = 2
 TURN_SLOTS = (0, 1)
 MM_BANKS = 4

from contextlib import ExitStack

import concourse.mybir as mybir
from concourse.masks import make_identity

FLOPS = 2 * 4096 * 512 * 1024

F32 = mybir.dt.float32
BF16 = mybir.dt.bfloat16
U32 = mybir.dt.uint32
U8 = mybir.dt.uint8
FP8X4 = mybir.dt.float8_e4m3fn_x4
FP8 = mybir.dt.float8_e4m3fn
ALU = mybir.AluOpType
ACT = mybir.ActivationFunctionType
AX = mybir.AxisListType

P = 128
K = 512
PACK = 4
N = 1024
BANK = 512
EPS = 1e-5
TILES = 32
QUAD = 4
QUADS = TILES // QUAD

W_VECTOR_COLS = 320
POOL_SCALES_FROM = 20
O_BUFS = 6
VECTOR_COLS = {9: 256, 10: 1024, 11: 704}
EARLY_POOL_SCALES = (0,)
FOLD_COPY = (2, 0)
MEAN_COPY = (2, 1)
HEAD_TURNS = (1, 2, 3)
FOLDED_A_QUAD = 3
AHEAD = 2
TURN_SLOTS = (0, 1)
MM_BANKS = 4
TURN_BANKS = 1
QUANTIZE_SLOT = 3
ADDS_BEFORE_PARK = 1
LATE_ADDS = (30, 31)
ADD_A = 26
ADD_B = 27
TAIL_FROM = 8
TAIL_SLOT = 3
TENSOR_BIAS = (0, 1, 2, 3)
FOLD_FROM = 8
LATE_UNTIL = 3


def tile_transformerblock_pb_t_kernel(tc, y_act, h, W2, b2, g2, out_0, out_1):
    nc = tc.nc
    y_quads = y_act.flatten_outer_dims().rearrange("(q p j) k -> q p j k", p=P, j=QUAD)
    h_quads = h.flatten_outer_dims().rearrange("(q p j) n -> q p j n", p=P, j=QUAD)
    out_0_quads = out_0.flatten_outer_dims().rearrange("(q p j) n -> q p j n", p=P, j=QUAD)
    out_1_quads = out_1.flatten_outer_dims().rearrange("(q p j) n -> q p j n", p=P, j=QUAD)

    groups = [[0], [1], [2, 3]] + [list(range(QUAD * q, QUAD * q + QUAD)) for q in range(1, 7)] + [[28, 29], [30], [31]]
    units = [(0, 1), (1, 2), (2, 4)] + [(QUAD * q, QUAD * q + QUAD) for q in range(1, QUADS)]
    unit_of = {}
    for u in range(len(units)):
        for i in range(units[u][0], units[u][1]):
            unit_of[i] = u

    pair_of = {}
    for group in groups:
        for k in range(len(group)):
            pair_of[group[k]] = group[k - k % 2]

    with ExitStack() as ctx:
        const = ctx.enter_context(tc.tile_pool(name="const", bufs=1))
        y_pool = ctx.enter_context(tc.tile_pool(name="y_pool", bufs=4))
        grouped_pool = ctx.enter_context(tc.tile_pool(name="grouped_pool", bufs=4))
        codes_pool = ctx.enter_context(tc.tile_pool(name="codes_pool", bufs=4))
        h_pool = ctx.enter_context(tc.tile_pool(name="h_pool", bufs=3))
        r_pool = ctx.enter_context(tc.tile_pool(name="r_pool", bufs=12))
        t_pool = ctx.enter_context(tc.tile_pool(name="t_pool", bufs=6))
        o_pool = ctx.enter_context(tc.tile_pool(name="o_pool", bufs=O_BUFS))
        bytes_pool = ctx.enter_context(tc.tile_pool(name="bytes_pool", bufs=5))
        squares_pool = ctx.enter_context(tc.tile_pool(name="squares_pool", bufs=2))
        g2_psum = ctx.enter_context(tc.psum_pool(name="g2_psum", bufs=1))
        mm_psum = ctx.enter_context(tc.psum_pool(name="mm_psum", bufs=MM_BANKS))
        turn_psum = ctx.enter_context(tc.psum_pool(name="turn_psum", bufs=TURN_BANKS))
        fold_psum = ctx.enter_context(tc.psum_pool(name="fold_psum", bufs=2))
        fold_pool = ctx.enter_context(tc.tile_pool(name="fold_pool", bufs=3))
        ctx.enter_context(tc.manual_schedule())

        y_rows = {}
        y_grouped = {}
        y_codes = {}
        y_scales = {}
        h_rows = {}
        r_tiles = {}
        t_pairs = {}
        byte_tiles = {}
        o_tiles = {}
        products = {}
        squared = []
        folded = {}
        folded_sbuf = {}

        half_sums = const.tile([P, 2 * TILES], F32, name="half_sums", tag="half_sums")
        duo = const.tile([P, 2, TILES], F32, name="duo", tag="duo")
        neg_mean = const.tile([P, TILES], F32, name="neg_mean", tag="neg_mean")
        sq_sums = const.tile([P, TILES], F32, name="sq_sums", tag="sq_sums")
        stats = const.tile([P, 5, TILES], F32, name="stats", tag="stats")
        factor = const.tile([P, TILES], F32, name="factor", tag="factor")
        unused_pair = const.tile([P, 2], F32, name="unused_pair", tag="unused_pair")

        def t_of(i):
            return t_pairs[pair_of[i]][:, i - pair_of[i], :]

        def span(g):
            return groups[g][0], groups[g][-1] + 1

        def load_y(u):
            a, z = units[u]
            y_rows[u] = y_pool.tile([P, z - a, K], BF16, name="y_rows", tag="y_rows")
            nc.sync.dma_start(out=y_rows[u][:], in_=y_quads[a // QUAD][:, a % QUAD : a % QUAD + z - a, :])

        def load_h(q, j0, j1):
            if j0 == 0:
                h_rows[q] = h_pool.tile([P, QUAD, N], BF16, name="h_rows", tag="h_rows")
            nc.sync.dma_start(out=h_rows[q][:, j0:j1, :], in_=h_quads[q][:, j0:j1, :])

        def turn_y(u, halves=(0, 1)):
            a, z = units[u]
            if 0 in halves:
                y_grouped[u] = grouped_pool.tile([P, QUAD * K], BF16, name="y_grouped", tag="y_grouped", align_bytes=64)
            for j0 in range(0, z - a, 2):
                if j0 // 2 not in halves:
                    continue
                nj = min(2, z - a - j0)
                if u in HEAD_TURNS:
                    turned = mm_psum.tile([P, 2, 2, P], F32, name="product", tag="product")
                else:
                    turned = turn_psum.tile([P, 2, 2, P], F32, name="turned", tag="turned")
                for j in range(nj):
                    words = y_rows[u][:, j0 + j, :].bitcast(F32)
                    for e in range(2):
                        nc.tensor.transpose(turned[:, j, e, :], words[:, e : K // 2 : 2], identity[:])
                nc.scalar.copy(
                    out=y_grouped[u][:, j0 * K : (j0 + nj) * K].bitcast(F32).rearrange("p (j r e) -> p j r e", j=nj, e=2),
                    in_=turned[:, 0:nj, :, :].rearrange("p j e r -> p j r e"),
                )

        def quantize_y(u):
            a, z = units[u]
            y_codes[u] = codes_pool.tile([P, QUAD * P], U32, name="y_codes", tag="y_codes", align_bytes=64)
            y_scales[u] = codes_pool.tile([P, QUAD * P], U8, name="y_scales", tag="y_scales", align_bytes=64)
            nc.vector.quantize_mx(
                out=y_codes[u][:, 0 : (z - a) * P].bitcast(FP8X4),
                scales=y_scales[u][:, 0 : (z - a) * P],
                in_=y_grouped[u][:, 0 : (z - a) * K],
            )

        def park_pool(u):
            nc.gpsimd.tensor_copy(out=parked[:, 0:1], in_=y_codes[u][:, 0:1])

        def add_bias(i):
            r_tiles[i] = r_pool.tile([P, N], F32, name="r_tile", tag="r_tile")
            nc.gpsimd.tensor_tensor(out=r_tiles[i][:], in0=h_rows[i // QUAD][:, i % QUAD, :], in1=b2_rows[:], op=ALU.add)

        def multiply(i, b):
            if (i, b) in products:
                return
            u = unit_of[i]
            rows = slice((i - units[u][0]) * P, (i - units[u][0] + 1) * P)
            cols = slice(b * BANK, (b + 1) * BANK)
            product = mm_psum.tile([P, BANK], F32, name="product", tag="product")
            products[(i, b)] = product
            nc.tensor.matmul_mx(
                out=product[:],
                lhsT=y_codes[u][:, rows].bitcast(FP8X4),
                lhsT_scale=y_scales[u][:, rows],
                rhs=w_codes[:, cols].bitcast(FP8X4),
                rhs_scale=w_scales[:, cols],
                start=True,
                stop=True,
            )

        def matmul_residual(i, b):
            multiply(i, b)
            product = products[(i, b)]
            cols = slice(b * BANK, (b + 1) * BANK)
            if folds(i):
                nc.vector.tensor_tensor(out=r_tiles[i][:, cols], in0=product[:], in1=r_tiles[i][:, cols], op=ALU.add)
            else:
                nc.vector.scalar_tensor_tensor(
                    out=r_tiles[i][:, cols],
                    in0=product[:],
                    scalar=1.0,
                    in1=r_tiles[i][:, cols],
                    op0=ALU.mult,
                    op1=ALU.add,
                    accum_out=half_sums[:, 2 * i + b : 2 * i + b + 1],
                )

        def folds(i):
            return FOLD_FROM <= i < TILES - QUAD and i % QUAD < FOLDED_A_QUAD

        def fold_rows(i):
            e = i % 2
            if e == 0:
                folded[i // 2] = fold_psum.tile([P, BANK], F32, name="folded", tag="folded")
            for c in range(N // P):
                nc.tensor.matmul(
                    out=folded[i // 2][:, e * P : (e + 1) * P], lhsT=r_tiles[i][:, c * P : (c + 1) * P], rhs=identity[:],
                    is_transpose=True, start=(c == 0), stop=(c == N // P - 1),
                )

        def copy_folds(pair):
            n = len([i for i in (2 * pair, 2 * pair + 1) if folds(i)])
            folded_sbuf[pair] = fold_pool.tile([P, 2 * P], F32, name="folded_sbuf", tag="folded_sbuf")
            nc.scalar.copy(out=folded_sbuf[pair][:, 0 : n * P], in_=folded[pair][:, 0 : n * P])
            for e in range(n):
                nc.tensor.matmul(
                    out=folded[pair][:, 2 * P + e : 2 * P + e + 1], lhsT=folded_sbuf[pair][:, e * P : (e + 1) * P],
                    rhs=minus_inv_n[:, 0:1], start=True, stop=True,
                )

        def copy_means(pair):
            n = len([i for i in (2 * pair, 2 * pair + 1) if folds(i)])
            nc.scalar.copy(out=neg_mean[:, 2 * pair : 2 * pair + n], in_=folded[pair][:, 2 * P : 2 * P + n])

        def unfolded(g):
            own = [i for i in groups[g] if not folds(i)]
            return (own[0], own[-1] + 1) if own else (0, 0)

        def early_mean(g):
            return 3 < g < len(groups) and len(groups[g]) == 1

        def add_half_sums(g):
            a, z = unfolded(g)
            if z - a > 1:
                nc.vector.tensor_reduce(
                    out=duo[:, 0, a:z],
                    in_=half_sums[:, 2 * a : 2 * z].rearrange("p (i b) -> p i b", b=2),
                    axis=AX.X,
                    op=ALU.add,
                )

        def negate_mean(g):
            a, z = unfolded(g)
            if z - a > 1:
                nc.vector.tensor_reduce(
                    out=neg_mean[:, a:z], in_=duo[:, :, a:z].rearrange("p c i -> p i c"), axis=AX.X, op=ALU.mult,
                )
            else:
                negate_mean_of(a)

        def negate_mean_of(i):
            nc.vector.tensor_scalar(
                out=unused_pair[:], in0=half_sums[:, 2 * i : 2 * i + 2], scalar1=-1.0 / N, scalar2=None, op0=ALU.mult,
                op1=ALU.add, accum_out=neg_mean[:, i : i + 1],
            )

        def square_deviation(i):
            squared.append(i)
            squares = squares_pool.tile([P, N], BF16, name="squares", tag="squares")
            nc.scalar.activation(
                out=squares[:], in_=r_tiles[i][:], func=ACT.Square, bias=neg_mean[:, i : i + 1], scale=1.0,
                accum_out=sq_sums[:, i : i + 1],
            )

        def root(g):
            a, z = span(g)
            nc.scalar.activation(out=stats[:, 1, a:z], in_=sq_sums[:, a:z], func=ACT.Sqrt, bias=EPS, scale=1.0 / N)

        def invert(g, rows=(0, 2)):
            a, z = span(g)
            if g >= TAIL_FROM and rows == (0, 2):
                rows = (0, 1)
            nc.vector.reciprocal(out=stats[:, 3 + rows[0] : 3 + rows[1], a:z], in_=stats[:, rows[0] : rows[1], a:z])

        def gain(i):
            if i == pair_of[i]:
                t_pairs[i] = t_pool.tile([P, 2, N], F32, name="t_pair", tag="t_pair", align_bytes=64)
            nc.vector.scalar_tensor_tensor(
                out=t_of(i), in0=r_tiles[i][:], scalar=neg_mean[:, i : i + 1], in1=g2_rows[:], op0=ALU.add, op1=ALU.mult,
            )

        def row_amax(first):
            n = len([i for i in range(TILES) if pair_of[i] == first])
            nc.vector.tensor_reduce(
                out=stats[:, 0, first : first + n], in_=t_pairs[first][:, 0:n, :], axis=AX.X, op=ALU.max, apply_absolute_value=True,
            )

        def scale_of_rows(g):
            a, z = span(g)
            nc.vector.tensor_reduce(out=factor[:, a:z], in_=stats[:, 2:4, a:z].rearrange("p c i -> p i c"), axis=AX.X, op=ALU.mult)

        def scale_on_pool(i):
            o_tiles[i] = o_pool.tile([P, N], F32, name="o_tile", tag="o_tile")
            nc.gpsimd.tensor_scalar(
                out=o_tiles[i][:], in0=t_of(i), scalar1=stats[:, 4, i : i + 1], scalar2=1.0, op0=ALU.mult, op1=ALU.mult,
            )

        def pool_scales(i):
            return (POOL_SCALES_FROM <= i) or (i >= QUAD and i % QUAD in EARLY_POOL_SCALES)

        def store_scaled(i):
            nc.sync.dma_start(out=out_0_quads[i // QUAD][:, i % QUAD, :], in_=o_tiles[i][:])

        def scale_and_store(g, i):
            if not pool_scales(i):
                o_tiles[i] = o_pool.tile([P, N], F32, name="o_tile", tag="o_tile")
                nc.scalar.activation(out=o_tiles[i][:], in_=t_of(i), func=ACT.Copy, scale=stats[:, 4, i : i + 1])
            if g < TAIL_FROM:
                store_scaled(i)

        def cast_and_store(g, i):
            a, z = span(g)
            t = t_of(i)
            c = VECTOR_COLS.get(g, 0)
            if i == a:
                byte_tiles[g] = bytes_pool.tile([P, z - a, N], FP8, name="byte_tile", tag="byte_tile")
            if c:
                nc.vector.tensor_scalar(
                    out=byte_tiles[g][:, i - a, 0:c], in0=t[:, 0:c], scalar1=factor[:, i : i + 1], scalar2=None, op0=ALU.mult,
                    saturate=False,
                )
            if c < N:
                nc.scalar.activation(
                    out=byte_tiles[g][:, i - a, c:N], in_=t[:, c:N], func=ACT.Identity, scale=factor[:, i : i + 1],
                    bias=zeros[:, 0:1], saturate=False,
                )
            if i == z - 1:
                nc.sync.dma_start(
                    out=out_1_quads[i // QUAD][:, a % QUAD : a % QUAD + z - a, :], in_=byte_tiles[g][:].bitcast(U8),
                )

        b2_vector = const.tile([P, N], BF16, name="b2_vector", tag="b2_vector")
        nc.vector.memset(b2_vector[:].bitcast(F32), 0.0)
        g2_vector = const.tile([P, N], BF16, name="g2_vector", tag="g2_vector")
        nc.gpsimd.memset(g2_vector[:].bitcast(F32), 0.0)
        ones = const.tile([P, P], BF16, name="ones", tag="ones")
        nc.vector.memset(ones[:], 1.0)
        zeros = const.tile([P, TILES], F32, name="zeros", tag="zeros")
        nc.vector.memset(zeros[:], 0.0)
        minus_inv_n = const.tile([P, 1], F32, name="minus_inv_n", tag="minus_inv_n")
        nc.vector.memset(minus_inv_n[:], -1.0 / N)
        one = const.tile([P, 1], F32, name="one", tag="one")
        nc.vector.memset(one[:], 1.0)
        warmed = const.tile([P, 1], F32, name="warmed", tag="warmed")
        nc.scalar.activation(out=warmed[:], in_=one[:], func=ACT.Sqrt)
        nc.vector.memset(stats[:, 2, :], 448.0)
        nc.vector.tensor_scalar(out=duo[:, 1, :], in0=zeros[:], scalar1=1.0, scalar2=-1.0 / N, op0=ALU.mult, op1=ALU.add)
        identity = const.tile([P, P], F32, name="identity", tag="identity")
        make_identity(nc, identity[:])
        identity_16 = const.tile([P, P], BF16, name="identity_16", tag="identity_16")
        make_identity(nc, identity_16[:])

        w_rows = []
        w_grouped = []
        w_rows_pair = t_pool.tile([P, 2, PACK, BANK], BF16, name="w_rows_pair", tag="t_pair", align_bytes=64)
        w_grouped_pair = t_pool.tile([P, 2, PACK * BANK], BF16, name="w_grouped_pair", tag="t_pair", align_bytes=64)
        for b in range(2):
            w_rows.append(w_rows_pair[:, b, :, :])
            w_grouped.append(w_grouped_pair[:, b, :])
        w_codes = const.tile([P, N], U32, name="w_codes", tag="w_codes", align_bytes=64)
        w_scales = const.tile([P, N], U8, name="w_scales", tag="w_scales", align_bytes=64)
        b2_rows = const.tile([P, N], BF16, name="b2_rows", tag="b2_rows")
        parked = const.tile([P, 1], U32, name="parked", tag="parked")
        w_view = W2.rearrange("(p j) n -> p j n", j=PACK)

        nc.sync.dma_start(out=w_rows[0], in_=w_view[:, :, 0:BANK])
        nc.sync.dma_start(out=b2_vector[0:1, :], in_=b2.rearrange("(o n) -> o n", o=1))
        nc.sync.dma_start(out=w_rows[1], in_=w_view[:, :, BANK:N])
        load_y(0)
        load_y(1)
        load_h(0, 0, 1)
        nc.sync.dma_start(out=g2_vector[0:1, :], in_=g2.rearrange("(o n) -> o n", o=1))
        load_h(0, 1, 2)
        load_y(2)
        load_h(0, 2, 4)
        load_h(1, 0, 4)
        load_y(3)
        load_y(4)

        b2_banks = []
        for b in range(2):
            b2_bank = fold_psum.tile([P, BANK], F32, name="folded", tag="folded")
            nc.tensor.matmul(out=b2_bank[:], lhsT=ones[:], rhs=b2_vector[:, b * BANK : (b + 1) * BANK], start=True, stop=True)
            b2_banks.append(b2_bank)
        g2_rows = g2_psum.tile([P, N], BF16, name="g2_rows", tag="g2_rows")

        def spread_g2():
            for b in range(2):
                nc.tensor.matmul(
                    out=g2_rows[:, b * BANK : (b + 1) * BANK],
                    lhsT=ones[:],
                    rhs=g2_vector[:, b * BANK : (b + 1) * BANK],
                    start=True,
                    stop=True,
                )

        def interleave_w(b):
            grouped = w_grouped[b].rearrange("p (c i j) -> p c j i", i=PACK, j=PACK)
            rows = w_rows[b].rearrange("p j (c i) -> p c j i", i=PACK)
            cut = W_VECTOR_COLS // PACK
            nc.vector.tensor_copy(out=grouped[:, 0:cut, :, :], in_=rows[:, 0:cut, :, :])
            nc.scalar.copy(out=grouped[:, cut : BANK // PACK, :, :], in_=rows[:, cut : BANK // PACK, :, :])

        def quantize_w(b):
            cols = slice(b * BANK, (b + 1) * BANK)
            nc.vector.quantize_mx(out=w_codes[:, cols].bitcast(FP8X4), scales=w_scales[:, cols], in_=w_grouped[b])

        def add_bias_on_tensor(i):
            r_tiles[i] = r_pool.tile([P, N], F32, name="r_tile", tag="r_tile")
            for b in range(2):
                cols = slice(b * BANK, (b + 1) * BANK)
                hb = mm_psum.tile([P, BANK], F32, name="product", tag="product")
                nc.tensor.matmul(out=hb[:], lhsT=ones[:], rhs=b2_vector[:, cols], start=True, stop=False)
                nc.tensor.matmul(out=hb[:], lhsT=identity_16[:], rhs=h_rows[0][:, i, cols], start=False, stop=True)
                nc.scalar.copy(out=r_tiles[i][:, cols], in_=hb[:])

        def add_bias_on_vector(i):
            r_tiles[i] = r_pool.tile([P, N], F32, name="r_tile", tag="r_tile")
            for b in range(2):
                cols = slice(b * BANK, (b + 1) * BANK)
                nc.vector.tensor_tensor(out=r_tiles[i][:, cols], in0=h_rows[0][:, i, cols], in1=b2_banks[b][:], op=ALU.add)

        interleave_w(0)
        quantize_w(0)
        interleave_w(1)
        turn_y(0)
        turn_y(1)
        quantize_y(0)
        quantize_w(1)
        quantize_y(1)
        for b in range(2):
            multiply(0, b)
        for b in range(2):
            nc.scalar.copy(out=b2_rows[:, b * BANK : (b + 1) * BANK], in_=b2_banks[b][:])
        add_bias_on_vector(0)
        add_bias(2)
        turn_y(2)
        spread_g2()
        matmul_residual(0, 0)
        matmul_residual(0, 1)
        add_bias_on_tensor(1)
        negate_mean(0)
        for b in range(2):
            multiply(1, b)
        gain(0)
        quantize_y(2)
        park_pool(2)
        add_bias(3)
        add_bias(4)
        matmul_residual(1, 0)
        matmul_residual(1, 1)
        square_deviation(0)
        for b in range(2):
            multiply(2, b)
        row_amax(0)
        negate_mean(1)
        gain(1)
        turn_y(3)
        root(0)
        for b in range(2):
            multiply(3, b)
        load_y(5)
        load_h(2, 0, QUAD)
        matmul_residual(2, 0)
        matmul_residual(2, 1)
        square_deviation(1)
        matmul_residual(3, 0)
        negate_mean_of(2)
        matmul_residual(3, 1)
        add_bias(5)
        row_amax(1)
        negate_mean_of(3)
        gain(2)
        turn_y(4)
        root(1)
        quantize_y(3)
        park_pool(3)
        add_bias(6)
        add_bias(7)
        for i in (4, 5):
            for b in range(2):
                multiply(i, b)
        invert(0)
        gain(3)
        scale_of_rows(0)
        scale_and_store(0, 0)
        cast_and_store(0, 0)

        for s in range(3, len(groups) + 2):
            entering = groups[s] if s < len(groups) else []
            middle = groups[s - 1] if 0 <= s - 1 < len(groups) else []
            leaving = groups[s - 2] if 0 <= s - 2 < len(groups) else []
            slots = max(len(entering), len(middle), len(leaving))
            u = unit_of[entering[0]] if entering else len(units)
            q = entering[0] // QUAD if entering else QUADS
            opens = bool(entering) and entering[0] == units[u][0] and u >= 2
            if opens and u + 3 < len(units):
                load_y(u + 3)
            if opens and q + 2 < QUADS:
                load_h(q + 2, 0, QUAD)
            to_turn = (u + 2 if opens and u + 2 < len(units) else 0)
            to_quantize = u + 1 if opens and u + 1 < len(units) else 0
            next_quad = [i for i in range(QUAD * (q + 1), QUAD * (q + 2)) if i not in r_tiles] if to_quantize else []
            late = s <= LATE_UNTIL
            before_park = ADDS_BEFORE_PARK

            if entering and s > 0:
                matmul_residual(entering[0], 0)
            if middle and s > 3 and not folds(middle[-1]) and not early_mean(s - 1):
                negate_mean(s - 1)
            if entering and s > 0:
                matmul_residual(entering[0], 1)
            if len(middle) == QUAD and folds(middle[2]):
                copy_folds(middle[2] // 2)
            if leaving and not late:
                invert(s - 2)
            for i in leaving:
                if pool_scales(i) and i not in o_tiles:
                    scale_on_pool(i)
            for i in middle:
                if folds(i) and i == middle[2]:
                    copy_means(i // 2)
                if i not in squared:
                    square_deviation(i)
            root_later = len(middle) == QUAD or (bool(leaving) and 0 < s - 1 < len(groups) - 1)
            if middle and (s - 1 == TAIL_FROM + 1 or not root_later) and not early_mean(s - 1):
                root(s - 1)
            for i in next_quad[0:before_park]:
                add_bias(i)
            if entering and entering[0] == TILES - QUAD:
                add_bias(30)
            behind = []
            for x in range(slots):
                if x < len(middle) and s > 3:
                    gain(middle[x])
                if x == 0 and leaving and not late:
                    scale_of_rows(s - 2)
                if x == 0 and early_mean(s):
                    negate_mean(s)
                    square_deviation(entering[0])
                    if s == len(groups) - 1:
                        root(s)
                if s - 1 >= TAIL_FROM and x == min(TAIL_SLOT, len(middle) - 1):
                    invert(s - 1, (1, 2))
                if s - 1 >= TAIL_FROM and min(TAIL_SLOT, len(middle) - 1) <= x < len(middle):
                    for i in middle[0 : x + 1]:
                        if i not in o_tiles:
                            scale_on_pool(i)
                            store_scaled(i)
                        if i == ADD_B and 31 not in r_tiles:
                            add_bias(31)
                if x == slots - 1 and leaving and late:
                    invert(s - 2)
                if to_quantize and x == min(QUANTIZE_SLOT, slots - 1):
                    quantize_y(to_quantize)
                    park_pool(to_quantize)
                    for i in next_quad[before_park:QUAD]:
                        if i not in LATE_ADDS:
                            add_bias(i)
                    for i in groups[s + 1][0:AHEAD]:
                        multiply(i, 0)
                        multiply(i, 1)
                for i in behind:
                    row_amax(i)
                behind = []
                if x + AHEAD < len(entering):
                    multiply(entering[x + AHEAD], 0)
                    multiply(entering[x + AHEAD], 1)
                if x + 1 < len(entering):
                    matmul_residual(entering[x + 1], 0)
                    matmul_residual(entering[x + 1], 1)
                if x < len(entering) and folds(entering[x]):
                    fold_rows(entering[x])
                if x in TURN_SLOTS and to_turn:
                    turn_y(to_turn, [h for h in (0, 1) if TURN_SLOTS[h] == x] if slots > 1 else (0, 1))
                if x == 0 and len(middle) == QUAD:
                    root(s - 1)
                if x < len(middle) and (x % 2 == 1 or x == len(middle) - 1):
                    behind = [pair_of[middle[x]]]
                if x == FOLD_COPY[0] and not FOLD_COPY[1] and entering and folds(entering[0]):
                    copy_folds(entering[0] // 2)
                if x == MEAN_COPY[0] and not MEAN_COPY[1] and entering and folds(entering[0]):
                    copy_means(entering[0] // 2)
                if x == slots - 1 and leaving and late:
                    scale_of_rows(s - 2)
                if x == 0 and leaving and not late:
                    scale_and_store(s - 2, leaving[0])
                if x + 1 < len(leaving) and not late:
                    scale_and_store(s - 2, leaving[x + 1])
                if x == slots - 1 and late:
                    for i in leaving:
                        scale_and_store(s - 2, i)
                        cast_and_store(s - 2, i)
                if VECTOR_COLS.get(s - 2, 0):
                    for i in behind:
                        row_amax(i)
                    behind = []
                if x < len(leaving) and not late:
                    cast_and_store(s - 2, leaving[x])
                if x == 0 and len(middle) < QUAD:
                    if root_later and s - 1 < TAIL_FROM:
                        root(s - 1)
                    if early_mean(s) and s < len(groups) - 1:
                        root(s)
                if x == FOLD_COPY[0] and FOLD_COPY[1] and entering and folds(entering[0]):
                    copy_folds(entering[0] // 2)
                if x == MEAN_COPY[0] and MEAN_COPY[1] and entering and folds(entering[0]):
                    copy_means(entering[0] // 2)
            for i in behind:
                row_amax(i)
            if entering and not folds(entering[-1]):
                add_half_sums(s)
